import numpy as np
import ml_dtypes


def mxq(x, axis, fmt="e4m3"):
    dtype, down = {"e4m3": (ml_dtypes.float8_e4m3fn, 7), "e5m2": (ml_dtypes.float8_e5m2, 14)}[fmt]
    v = np.moveaxis(np.asarray(x, np.float32).astype(ml_dtypes.bfloat16).astype(np.float64), axis, -1)
    blocks = v.reshape(v.shape[:-1] + (-1, 32))
    amax = np.abs(blocks).max(-1, keepdims=True)
    byte = np.maximum(np.where(amax > 0, np.frexp(amax)[1] - 1 + 127, 0) - down, 1)
    scale = np.exp2(byte - 127.0)
    codes = (blocks / scale).astype(np.float32).astype(dtype).astype(np.float64)
    return np.moveaxis((codes * scale).reshape(v.shape), -1, axis)


WIDE = False


def mx_kscale(k):
    if not WIDE:
        return np.ones(k)
    levels = np.array([10, -10, 5, -5, 0])
    if k % 512:
        return np.exp2(np.random.permutation(np.resize(levels, k // 32))).repeat(32)
    a = np.empty((k // 512, 16))
    for p in range(k // 512):
        a[p, :8] = np.random.permutation(np.resize(levels, 8))
        for g in range(8):
            far = levels[np.abs(levels - a[p, g]) >= 10]
            a[p, g + 8] = far[np.random.randint(len(far))]
    return np.exp2(a.ravel()).repeat(32)


BF16 = ml_dtypes.bfloat16


def bf(x):
    return np.asarray(x, np.float32).astype(BF16)


def f64(x):
    return np.asarray(x).astype(np.float64)


B, S, DIM, H, NOPE, ROPE_SP, V_SP, KV_RANK = 2, 256, 2048, 16, 64, 128, 128, 512
C = 1.0
QK_SP = NOPE + ROPE_SP


def lift(sp):
    return np.concatenate([np.sqrt((sp * sp).sum(-1, keepdims=True) + C), sp], -1)


def rope(u, cos, sin):
    u1, u2 = u[..., 0::2], u[..., 1::2]
    cos, sin = cos[None, :, None, :], sin[None, :, None, :]
    return np.stack([u1 * cos - u2 * sin, u1 * sin + u2 * cos], -1).reshape(u.shape)


def setup_inputs():
    s = mx_kscale(DIM)
    inv = 1.0 / (10000.0 ** (np.arange(0, ROPE_SP, 2) / ROPE_SP))
    ang = np.arange(S)[:, None] * inv[None, :]
    return {"x": bf(np.random.standard_normal((B, S, DIM)) * s),
            "freqs_cos": bf(np.cos(ang)),
            "freqs_sin": bf(np.sin(ang)),
            "wq_w": bf(np.random.standard_normal((H * QK_SP, DIM)) * 0.3 / np.sqrt(DIM) / s[None, :]),
            "wq_b": bf(np.random.standard_normal(H * QK_SP) * 0.1)}


def core(x, freqs_cos, freqs_sin, wq_w, wq_b):
    q = (mxq(f64(x), 2, "e4m3") @ mxq(f64(wq_w), 1, "e4m3").T) + f64(wq_b)
    q = q.reshape(B, S, H, QK_SP)
    q_nope, q_pe = q[..., :NOPE], q[..., NOPE:]
    q_pe = rope(q_pe, f64(freqs_cos), f64(freqs_sin))
    return lift(np.concatenate([q_nope, q_pe], -1))


def e4m3fn_bytes(y):
    return np.clip(np.asarray(y, np.float64), -448.0, 448.0).astype(np.float32).astype(ml_dtypes.float8_e4m3fn).view(np.uint8)


def reference(x, freqs_cos, freqs_sin, wq_w, wq_b):
    out = core(x, freqs_cos, freqs_sin, wq_w, wq_b)
    s = np.max(np.abs(out)) / 448.0
    return out, e4m3fn_bytes(out / s)

@@ -1,0 +1,255 @@
+from contextlib import ExitStack
+
+import concourse.mybir as mybir
+from concourse.masks import make_identity
+
+F32 = mybir.dt.float32
+BF16 = mybir.dt.bfloat16
+U32 = mybir.dt.uint32
+U8 = mybir.dt.uint8
+FP8X4 = mybir.dt.float8_e4m3fn_x4
+FP8 = mybir.dt.float8_e4m3fn
+ALU = mybir.AluOpType
+ACT = mybir.ActivationFunctionType
+AX = mybir.AxisListType
+
+P = 128
+K = 2048
+TOK = 512
+H = 16
+NOPE = 64
+ROPE = 128
+QK = NOPE + ROPE
+HD = QK + 1
+PASSES = 4
+FLOPS = 2 * TOK * H * QK * K
+
+CHUNKS = (("pe", 0), ("no", 0), ("pe", 1), ("pe", 2), ("no", 1), ("pe", 3))
+GROUP_DONE = {1: 0, 2: 1, 4: 2, 5: 3}
+RAW_BUFS = 10
+SQ_DELAY = 2
+V_SPLIT = 2048
+
+
+def tile_lorentzmla_pb_kernel(tc, x, freqs_cos, freqs_sin, wq_w, wq_b, out_0, out_1):
+    nc = tc.nc
+    xf = x.rearrange("b s k -> (b s) k")
+    wv = wq_w.rearrange("(h d) k -> h d k", d=QK)
+    o0 = out_0.rearrange("b s h d -> (b s) h d")
+    o1 = out_1.rearrange("b s h d -> (b s) (h d)")
+
+    with ExitStack() as ctx:
+        const = ctx.enter_context(tc.tile_pool(name="const", bufs=1))
+        rawp = ctx.enter_context(tc.tile_pool(name="rawp", bufs=RAW_BUFS))
+        gwp = ctx.enter_context(tc.tile_pool(name="gwp", bufs=2))
+        cdp = ctx.enter_context(tc.tile_pool(name="cdp", bufs=3))
+        tmp = ctx.enter_context(tc.tile_pool(name="tmp", bufs=4))
+        ps_t = ctx.enter_context(tc.psum_pool(name="ps_t", bufs=4))
+        ps_a = ctx.enter_context(tc.psum_pool(name="ps_a", bufs=4))
+        ctx.enter_context(tc.manual_schedule())
+
+        ident = const.tile([P, P], F32, name="ident")
+        make_identity(nc, ident[:])
+        one1 = const.tile([P, 1], F32, name="one1")
+        nc.vector.memset(one1[:], 1.0)
+        zero1 = const.tile([P, 1], F32, name="zero1")
+        nc.vector.memset(zero1[:], 0.0)
+        warm = const.tile([P, 1], F32, name="warm")
+        nc.scalar.activation(out=warm[:], in_=one1[:], func=ACT.Sqrt)
+
+        cos16 = const.tile([P, 2, 64], BF16, name="cos16")
+        sin16 = const.tile([P, 2, 64], BF16, name="sin16")
+        nc.scalar.dma_start(out=cos16[:], in_=freqs_cos.rearrange("(a p) j -> p a j", p=P))
+        nc.scalar.dma_start(out=sin16[:], in_=freqs_sin.rearrange("(a p) j -> p a j", p=P))
+        bias = const.tile([P, H, QK], BF16, name="bias")
+        biasf = bias[:].rearrange("p h d -> p (h d)")
+        nc.scalar.dma_start(out=biasf[:, 0:768], in_=wq_b[0:768].partition_broadcast(P))
+
+        c2 = const.tile([P, 2, 64, 2], F32, name="c2")
+        sn = const.tile([P, 2, 2, 64], F32, name="sn")
+        nc.vector.tensor_copy(out=c2[:], in_=cos16[:].unsqueeze(3).to_broadcast([P, 2, 64, 2]))
+        nc.vector.tensor_scalar(out=sn[:, :, 0, :], in0=sin16[:], scalar1=-1.0, scalar2=None, op0=ALU.mult)
+        nc.vector.tensor_copy(out=sn[:, :, 1, :], in_=sin16[:])
+
+        res = const.tile([P, 4, H, HD], F32, name="res")
+        res8 = const.tile([P, 4, H * HD], FP8, name="res8")
+        ssq = const.tile([P, 4, H], F32, name="ssq")
+        x_codes = const.tile([P, PASSES, TOK], U32, name="x_codes", align_bytes=64)
+        x_scales = const.tile([P, PASSES, TOK], U8, name="x_scales", align_bytes=64)
+
+        row_tiles = [("x", m) for m in range(4)]
+        for kind, i in CHUNKS:
+            row_tiles.extend([(kind, 4 * i + r) for r in range(4)])
+        raw = {}
+        banks = {}
+        grouped = {}
+        codes = {-1: (x_codes, x_scales)}
+        acc = {}
+
+        def load(k):
+            kind, i = row_tiles[k]
+            t = rawp.tile([P, K], BF16, name="raw", tag="raw")
+            raw[k] = t
+            if kind == "x":
+                nc.sync.dma_start(out=t[:], in_=xf[P * i : P * (i + 1), :])
+            elif kind == "pe":
+                nc.sync.dma_start(out=t[:], in_=wv[i, NOPE:QK, :])
+            else:
+                nc.sync.dma_start(out=t[0:64, :], in_=wv[2 * i, 0:NOPE, :])
+                nc.sync.dma_start(out=t[64:128, :], in_=wv[2 * i + 1, 0:NOPE, :])
+
+        def transposes(k):
+            words = raw[k][:].bitcast(F32)
+            banks[k] = []
+            for half in range(2):
+                xt = ps_t.tile([P, 2, 2, P], F32, name="xt", tag="xt")
+                for a in range(2):
+                    g = 2 * half + a
+                    for u in range(2):
+                        nc.tensor.transpose(xt[:, a, u, :], words[:, 256 * g + u : 256 * (g + 1) : 2], ident[:])
+                banks[k].append(xt)
+
+        def copies(k):
+            cc = k // 4 - 1
+            r = k % 4
+            if r == 0:
+                grouped[cc] = gwp.tile([P, PASSES, TOK, 4], BF16, name="grouped", tag="grouped", align_bytes=64)
+            for half in range(2):
+                nc.scalar.copy(
+                    out=grouped[cc][:, 2 * half : 2 * half + 2, P * r : P * (r + 1), :].bitcast(F32),
+                    in_=banks[k][half][:].rearrange("p a u r -> p a r u"),
+                )
+
+        def quantize(cc):
+            if cc >= 0:
+                wc = cdp.tile([P, PASSES, TOK], U32, name="w_codes", tag="w_codes", align_bytes=64)
+                ws = cdp.tile([P, PASSES, TOK], U8, name="w_scales", tag="w_scales", align_bytes=64)
+                codes[cc] = (wc, ws)
+            cd, sc = codes[cc]
+            for g in range(PASSES):
+                nc.vector.quantize_mx(
+                    out=cd[:, g, :].bitcast(FP8X4),
+                    scales=sc[:, g, :],
+                    in_=grouped[cc][:, g, :, :].rearrange("p n t -> p (n t)"),
+                )
+
+        def matmuls(cc, m):
+            wc, ws = codes[cc]
+            a = ps_a.tile([P, TOK], F32, name="acc", tag="acc")
+            acc[(cc, m)] = a
+            for g in range(PASSES):
+                nc.tensor.matmul_mx(
+                    out=a[:],
+                    lhsT=x_codes[:, g, P * m : P * (m + 1)].bitcast(FP8X4),
+                    lhsT_scale=x_scales[:, g, P * m : P * (m + 1)],
+                    rhs=wc[:, g, :].bitcast(FP8X4),
+                    rhs_scale=ws[:, g, :],
+                    start=(g == 0),
+                    stop=(g == PASSES - 1),
+                )
+
+        def epilogue(cc, ms):
+            kind, i = CHUNKS[cc]
+            if kind == "no":
+                for m in ms:
+                    nc.vector.tensor_tensor(
+                        out=res[:, m, 8 * i : 8 * i + 8, 1 : 1 + NOPE],
+                        in0=acc[(cc, m)][:].rearrange("p (h d) -> p h d", d=NOPE),
+                        in1=bias[:, 8 * i : 8 * i + 8, 0:NOPE],
+                        op=ALU.add,
+                    )
+                return
+            av = {}
+            t2 = {}
+            dst = {}
+            for m in ms:
+                av[m] = tmp.tile([P, 4, 64, 2], F32, name="av", tag="av")
+                t2[m] = tmp.tile([P, 2, 4, 64], F32, name="t2", tag="t2")
+                dst[m] = res[:, m, 4 * i : 4 * i + 4, 1 + NOPE : HD]
+                nc.vector.tensor_tensor(
+                    out=av[m][:].rearrange("p h j e -> p h (j e)"),
+                    in0=acc[(cc, m)][:].rearrange("p (h d) -> p h d", d=ROPE),
+                    in1=bias[:, 4 * i : 4 * i + 4, NOPE:QK],
+                    op=ALU.add,
+                )
+            for m in ms:
+                nc.vector.tensor_tensor(
+                    out=dst[m],
+                    in0=av[m][:].rearrange("p h j e -> p h (j e)"),
+                    in1=c2[:, m % 2].rearrange("p j e -> p (j e)").unsqueeze(1).to_broadcast([P, 4, ROPE]),
+                    op=ALU.mult,
+                )
+            for e in range(2):
+                for m in ms:
+                    nc.vector.tensor_tensor(
+                        out=t2[m][:, e, :, :],
+                        in0=av[m][:, :, :, 1 - e],
+                        in1=sn[:, m % 2, e, :].unsqueeze(1).to_broadcast([P, 4, 64]),
+                        op=ALU.mult,
+                    )
+            for m in ms:
+                d4 = dst[m].rearrange("p h (j e) -> p h j e", e=2)
+                nc.vector.tensor_tensor(out=d4, in0=d4, in1=t2[m][:].rearrange("p e h j -> p h j e"), op=ALU.add)
+
+        def squares(gq, ms):
+            for m in ms:
+                for h in range(4 * gq, 4 * gq + 4):
+                    junk = tmp.tile([P, QK], F32, name="junk", tag="junk")
+                    nc.scalar.activation(out=junk[:], in_=res[:, m, h, 1:HD], func=ACT.Square, accum_out=ssq[:, m, h : h + 1])
+            for m in ms:
+                nc.scalar.activation(out=res[:, m, 4 * gq : 4 * gq + 4, 0], in_=ssq[:, m, 4 * gq : 4 * gq + 4], func=ACT.Sqrt, bias=1.0)
+                nc.scalar.dma_start(out=o0[P * m : P * (m + 1), 4 * gq : 4 * gq + 4, :], in_=res[:, m, 4 * gq : 4 * gq + 4, :])
+
+        n_rt = len(row_tiles)
+        n_runs = n_rt // 2
+        for k in range(RAW_BUFS):
+            load(k)
+        pending = {}
+        for s in range(n_runs + 2 + SQ_DELAY):
+            if s < n_runs:
+                for k in (2 * s, 2 * s + 1):
+                    transposes(k)
+                for k in (2 * s, 2 * s + 1):
+                    copies(k)
+                    if k + RAW_BUFS < n_rt:
+                        load(k + RAW_BUFS)
+                if s == 2:
+                    nc.scalar.dma_start(out=biasf[:, 768 : H * QK], in_=wq_b[768 : H * QK].partition_broadcast(P))
+                if s % 2 == 1:
+                    quantize(s // 2 - 1)
+            q = s - 4
+            if 0 <= q < 12:
+                cc = q // 2
+                ms = (2 * (q % 2), 2 * (q % 2) + 1)
+                for m in ms:
+                    matmuls(cc, m)
+                epilogue(cc, ms)
+                if cc in GROUP_DONE:
+                    pending[s + SQ_DELAY] = (GROUP_DONE[cc], ms)
+            if s in pending:
+                squares(pending[s][0], pending[s][1])
+
+        pmax = const.tile([P, 1], F32, name="pmax")
+        nc.vector.tensor_reduce(out=pmax[:], in_=res[:].rearrange("p m h d -> p (m h) d")[:, :, 0], axis=AX.X, op=ALU.max)
+        spread = ps_t.tile([P, P], F32, name="spread", tag="xt")
+        nc.tensor.transpose(spread[:], pmax[:, 0:1].to_broadcast([P, P]), ident[:])
+        amax = const.tile([P, 1], F32, name="amax")
+        nc.vector.tensor_reduce(out=amax[:], in_=spread[:], axis=AX.X, op=ALU.max)
+        rcp = const.tile([P, 1], F32, name="rcp")
+        nc.vector.reciprocal(out=rcp[:], in_=amax[:])
+        fac = const.tile([P, 1], F32, name="fac")
+        nc.vector.tensor_scalar(out=fac[:], in0=rcp[:], scalar1=448.0, scalar2=None, op0=ALU.mult)
+        resf = res[:].rearrange("p m h d -> p m (h d)")
+        for m in range(4):
+            nc.vector.tensor_scalar(
+                out=res8[:, m, 0:V_SPLIT], in0=resf[:, m, 0:V_SPLIT], scalar1=fac[:, 0:1], scalar2=None, op0=ALU.mult, saturate=False
+            )
+            nc.scalar.activation(
+                out=res8[:, m, V_SPLIT : H * HD],
+                in_=resf[:, m, V_SPLIT : H * HD],
+                func=ACT.Identity,
+                scale=fac[:, 0:1],
+                bias=zero1[:, 0:1],
+                saturate=False,
+            )
+            nc.sync.dma_start(out=o1[P * m : P * (m + 1), :], in_=res8[:, m, :].bitcast(U8))

@@ -15,222 +15,287 @@ AX = mybir.AxisListType
 
 P = 128
 K = 2048
+KW = K // 2
 TOK = 512
+NT = 4
 H = 16
 NOPE = 64
 ROPE = 128
 QK = NOPE + ROPE
 HD = QK + 1
+ROW = H * HD
 PASSES = 4
 FLOPS = 2 * TOK * H * QK * K
 
-CHUNKS = (("pe", 0), ("no", 0), ("pe", 1), ("pe", 2), ("no", 1), ("pe", 3))
-GROUP_DONE = {1: 0, 2: 1, 4: 2, 5: 3}
+NCH = 8
+CW = 2 * QK
+N_A = 256
 RAW_BUFS = 10
-SQ_DELAY = 2
+WARM = 6
+HEAD_DUMMIES = 2
+SORT_AHEAD = 3
 V_SPLIT = 2048
+
+HEAD = (("x", 0), ("w", 0), ("w", 1), ("w", 2), ("x", 1), ("x", 2), ("x", 3))
+T_PLAN = ((), (3,), (4,), (5,)), ((6,), (7,), (8,), ())
+
+
+def t_plan(c, i):
+    if c < 2:
+        return T_PLAN[c][i]
+    if c == NCH - 1 or i == 3:
+        return ()
+    return (3 * c + 3 + i,)
 
 
 def tile_lorentzmla_pb_kernel(tc, x, freqs_cos, freqs_sin, wq_w, wq_b, out_0, out_1):
     nc = tc.nc
-    xf = x.rearrange("b s k -> (b s) k")
-    wv = wq_w.rearrange("(h d) k -> h d k", d=QK)
-    o0 = out_0.rearrange("b s h d -> (b s) h d")
-    o1 = out_1.rearrange("b s h d -> (b s) (h d)")
+    xv = x.rearrange("b s k -> (b s) k").rearrange("(p i) k -> p i k", i=NT)
+    o0 = out_0.rearrange("b s h d -> (b s) (h d)").rearrange("(p i) e -> p i e", i=NT)
+    o1 = out_1.rearrange("b s h d -> (b s) (h d)").rearrange("(p i) e -> p (i e)", i=NT)
+    cosv = freqs_cos.rearrange("(q i) j -> q i j", i=NT)
+    sinv = freqs_sin.rearrange("(q i) j -> q i j", i=NT)
 
     with ExitStack() as ctx:
         const = ctx.enter_context(tc.tile_pool(name="const", bufs=1))
         rawp = ctx.enter_context(tc.tile_pool(name="rawp", bufs=RAW_BUFS))
+        prm = ctx.enter_context(tc.tile_pool(name="prm", bufs=4))
         gwp = ctx.enter_context(tc.tile_pool(name="gwp", bufs=2))
         cdp = ctx.enter_context(tc.tile_pool(name="cdp", bufs=3))
-        tmp = ctx.enter_context(tc.tile_pool(name="tmp", bufs=4))
+        tmp = ctx.enter_context(tc.tile_pool(name="tmp", bufs=3))
         ps_t = ctx.enter_context(tc.psum_pool(name="ps_t", bufs=4))
         ps_a = ctx.enter_context(tc.psum_pool(name="ps_a", bufs=4))
         ctx.enter_context(tc.manual_schedule())
 
+        dummy = const.tile([P, TOK], BF16, name="dummy")
+        nc.vector.memset(dummy[:], 0.0)
         ident = const.tile([P, P], F32, name="ident")
         make_identity(nc, ident[:])
         one1 = const.tile([P, 1], F32, name="one1")
         nc.vector.memset(one1[:], 1.0)
         zero1 = const.tile([P, 1], F32, name="zero1")
         nc.vector.memset(zero1[:], 0.0)
+
+        cos16 = const.tile([P, NT, 64], BF16, name="cos16")
+        sin16 = const.tile([P, NT, 64], BF16, name="sin16")
+        for half in range(2):
+            nc.scalar.dma_start(out=cos16[64 * half : 64 * half + 64], in_=cosv)
+            nc.scalar.dma_start(out=sin16[64 * half : 64 * half + 64], in_=sinv)
         warm = const.tile([P, 1], F32, name="warm")
         nc.scalar.activation(out=warm[:], in_=one1[:], func=ACT.Sqrt)
-
-        cos16 = const.tile([P, 2, 64], BF16, name="cos16")
-        sin16 = const.tile([P, 2, 64], BF16, name="sin16")
-        nc.scalar.dma_start(out=cos16[:], in_=freqs_cos.rearrange("(a p) j -> p a j", p=P))
-        nc.scalar.dma_start(out=sin16[:], in_=freqs_sin.rearrange("(a p) j -> p a j", p=P))
         bias = const.tile([P, H, QK], BF16, name="bias")
         biasf = bias[:].rearrange("p h d -> p (h d)")
-        nc.scalar.dma_start(out=biasf[:, 0:768], in_=wq_b[0:768].partition_broadcast(P))
 
-        c2 = const.tile([P, 2, 64, 2], F32, name="c2")
-        sn = const.tile([P, 2, 2, 64], F32, name="sn")
-        nc.vector.tensor_copy(out=c2[:], in_=cos16[:].unsqueeze(3).to_broadcast([P, 2, 64, 2]))
-        nc.vector.tensor_scalar(out=sn[:, :, 0, :], in0=sin16[:], scalar1=-1.0, scalar2=None, op0=ALU.mult)
-        nc.vector.tensor_copy(out=sn[:, :, 1, :], in_=sin16[:])
+        c2 = const.tile([P, NT, 64, 2], F32, name="c2")
+        sn = const.tile([P, NT, 2, 64], F32, name="sn")
 
-        res = const.tile([P, 4, H, HD], F32, name="res")
-        res8 = const.tile([P, 4, H * HD], FP8, name="res8")
-        ssq = const.tile([P, 4, H], F32, name="ssq")
-        x_codes = const.tile([P, PASSES, TOK], U32, name="x_codes", align_bytes=64)
-        x_scales = const.tile([P, PASSES, TOK], U8, name="x_scales", align_bytes=64)
+        res = const.tile([P, NT, H, HD], F32, name="res")
+        resf = res[:].rearrange("p i h d -> p i (h d)")
+        res8 = const.tile([P, NT * ROW], FP8, name="res8")
+        ssq = const.tile([P, NT, H], F32, name="ssq")
+        x_codes = const.tile([P, NT, PASSES, P], U32, name="x_codes", align_bytes=64)
+        x_scales = const.tile([P, NT, PASSES, P], U8, name="x_scales", align_bytes=64)
 
-        row_tiles = [("x", m) for m in range(4)]
-        for kind, i in CHUNKS:
-            row_tiles.extend([(kind, 4 * i + r) for r in range(4)])
+        order = list(HEAD) + [("w", r) for r in range(3, 3 * NCH)]
         raw = {}
+        sorted_tiles = {}
         banks = {}
         grouped = {}
-        codes = {-1: (x_codes, x_scales)}
+        codes = {}
         acc = {}
+        state = {"loaded": 0, "prev": None, "summed": 0}
+        pending = []
 
-        def load(k):
-            kind, i = row_tiles[k]
+        def load():
+            n = state["loaded"]
+            if n >= len(order):
+                return
+            state["loaded"] = n + 1
+            kind, r = order[n]
             t = rawp.tile([P, K], BF16, name="raw", tag="raw")
-            raw[k] = t
-            if kind == "x":
-                nc.sync.dma_start(out=t[:], in_=xf[P * i : P * (i + 1), :])
-            elif kind == "pe":
-                nc.sync.dma_start(out=t[:], in_=wv[i, NOPE:QK, :])
+            raw[(kind, r)] = t
+            if n == 0:
+                nc.sync.dma_start(out=t[:, 0 : K // 2], in_=xv[:, r, 0 : K // 2])
+                nc.sync.dma_start(out=t[:, K // 2 : K], in_=xv[:, r, K // 2 : K])
+            elif kind == "x":
+                nc.sync.dma_start(out=t[:], in_=xv[:, r, :])
             else:
-                nc.sync.dma_start(out=t[0:64, :], in_=wv[2 * i, 0:NOPE, :])
-                nc.sync.dma_start(out=t[64:128, :], in_=wv[2 * i + 1, 0:NOPE, :])
+                nc.sync.dma_start(out=t[:], in_=wq_w[P * r : P * (r + 1), :])
 
-        def transposes(k):
-            words = raw[k][:].bitcast(F32)
-            banks[k] = []
+        def dummies(n):
+            for d in range(n):
+                sink = ps_a.tile([P, TOK], F32, name="sink", tag="acc")
+                nc.tensor.matmul(out=sink[:], lhsT=dummy[:, 0:P], rhs=dummy[:], start=True, stop=True)
+
+        def sort_words(t):
+            srt = prm.tile([P, 2, KW // 2], F32, name="srt", tag="srt")
+            nc.vector.tensor_copy(out=srt[:], in_=raw[t][:].bitcast(F32).rearrange("p (w u) -> p u w", u=2))
+            sorted_tiles[t] = srt
+
+        def transposes(t):
+            words = raw[t][:].bitcast(F32)
+            sorted_words = t in sorted_tiles
+            banks[t] = []
             for half in range(2):
                 xt = ps_t.tile([P, 2, 2, P], F32, name="xt", tag="xt")
                 for a in range(2):
                     g = 2 * half + a
                     for u in range(2):
-                        nc.tensor.transpose(xt[:, a, u, :], words[:, 256 * g + u : 256 * (g + 1) : 2], ident[:])
-                banks[k].append(xt)
+                        if sorted_words:
+                            src = sorted_tiles[t][:, u, P * g : P * (g + 1)]
+                        else:
+                            src = words[:, 256 * g + u : 256 * (g + 1) : 2]
+                        nc.tensor.transpose(xt[:, a, u, :], src, ident[:])
+                banks[t].append(xt)
+            load()
 
-        def copies(k):
-            cc = k // 4 - 1
-            r = k % 4
-            if r == 0:
-                grouped[cc] = gwp.tile([P, PASSES, TOK, 4], BF16, name="grouped", tag="grouped", align_bytes=64)
+        def quantize_x(i):
+            nc.vector.quantize_mx(
+                out=x_codes[:, i].rearrange("p g n -> p (g n)").bitcast(FP8X4),
+                scales=x_scales[:, i].rearrange("p g n -> p (g n)"),
+                in_=grouped[("x", i)][:].rearrange("p g n t -> p (g n t)"),
+            )
+
+        def quantize_w(c):
+            wc = cdp.tile([P, PASSES, CW], U32, name="w_codes", tag="w_codes", align_bytes=64)
+            ws = cdp.tile([P, PASSES, CW], U8, name="w_scales", tag="w_scales", align_bytes=64)
+            codes[c] = (wc, ws)
+            gin = grouped[("w", c)][:].rearrange("p g n t -> p (g n t)")
+            cf = wc[:].rearrange("p g n -> p (g n)")
+            sf = ws[:].rearrange("p g n -> p (g n)")
+            for lo, hi in ((0, 1024), (1024, PASSES * CW)):
+                nc.vector.quantize_mx(out=cf[:, lo:hi].bitcast(FP8X4), scales=sf[:, lo:hi], in_=gin[:, 4 * lo : 4 * hi])
+
+        def copies(t):
+            kind, r = t
+            if kind == "x":
+                key, col = ("x", r), 0
+                grouped[key] = gwp.tile([P, PASSES, P, 4], BF16, name="gx", tag="gx", align_bytes=64)
+            else:
+                key, col = ("w", r // 3), P * (r % 3)
+                if r % 3 == 0:
+                    grouped[key] = gwp.tile([P, PASSES, CW, 4], BF16, name="gw", tag="gw", align_bytes=64)
             for half in range(2):
                 nc.scalar.copy(
-                    out=grouped[cc][:, 2 * half : 2 * half + 2, P * r : P * (r + 1), :].bitcast(F32),
-                    in_=banks[k][half][:].rearrange("p a u r -> p a r u"),
+                    out=grouped[key][:, 2 * half : 2 * half + 2, col : col + P, :].bitcast(F32),
+                    in_=banks[t][half][:].rearrange("p a u r -> p a r u"),
                 )
+            if kind == "x":
+                quantize_x(r)
+            elif r % 3 == 2:
+                quantize_w(r // 3)
 
-        def quantize(cc):
-            if cc >= 0:
-                wc = cdp.tile([P, PASSES, TOK], U32, name="w_codes", tag="w_codes", align_bytes=64)
-                ws = cdp.tile([P, PASSES, TOK], U8, name="w_scales", tag="w_scales", align_bytes=64)
-                codes[cc] = (wc, ws)
-            cd, sc = codes[cc]
-            for g in range(PASSES):
-                nc.vector.quantize_mx(
-                    out=cd[:, g, :].bitcast(FP8X4),
-                    scales=sc[:, g, :],
-                    in_=grouped[cc][:, g, :, :].rearrange("p n t -> p (n t)"),
-                )
-
-        def matmuls(cc, m):
-            wc, ws = codes[cc]
-            a = ps_a.tile([P, TOK], F32, name="acc", tag="acc")
-            acc[(cc, m)] = a
-            for g in range(PASSES):
-                nc.tensor.matmul_mx(
-                    out=a[:],
-                    lhsT=x_codes[:, g, P * m : P * (m + 1)].bitcast(FP8X4),
-                    lhsT_scale=x_scales[:, g, P * m : P * (m + 1)],
-                    rhs=wc[:, g, :].bitcast(FP8X4),
-                    rhs_scale=ws[:, g, :],
-                    start=(g == 0),
-                    stop=(g == PASSES - 1),
-                )
-
-        def epilogue(cc, ms):
-            kind, i = CHUNKS[cc]
-            if kind == "no":
-                for m in ms:
-                    nc.vector.tensor_tensor(
-                        out=res[:, m, 8 * i : 8 * i + 8, 1 : 1 + NOPE],
-                        in0=acc[(cc, m)][:].rearrange("p (h d) -> p h d", d=NOPE),
-                        in1=bias[:, 8 * i : 8 * i + 8, 0:NOPE],
-                        op=ALU.add,
+        def matmuls(c, i):
+            wc, ws = codes[c]
+            a = ps_a.tile([P, CW], F32, name="acc", tag="acc")
+            acc[(c, i)] = a
+            for lo, hi in ((0, N_A), (N_A, CW)):
+                for g in range(PASSES):
+                    nc.tensor.matmul_mx(
+                        out=a[:, lo:hi],
+                        lhsT=x_codes[:, i, g, :].bitcast(FP8X4),
+                        lhsT_scale=x_scales[:, i, g, :],
+                        rhs=wc[:, g, lo:hi].bitcast(FP8X4),
+                        rhs_scale=ws[:, g, lo:hi],
+                        start=(g == 0),
+                        stop=(g == PASSES - 1),
                     )
-                return
-            av = {}
-            t2 = {}
-            dst = {}
-            for m in ms:
-                av[m] = tmp.tile([P, 4, 64, 2], F32, name="av", tag="av")
-                t2[m] = tmp.tile([P, 2, 4, 64], F32, name="t2", tag="t2")
-                dst[m] = res[:, m, 4 * i : 4 * i + 4, 1 + NOPE : HD]
+
+        def add_bias(c, i):
+            nc.vector.tensor_tensor(
+                out=res[:, i, 2 * c : 2 * c + 2, 1:HD],
+                in0=acc[(c, i)][:].rearrange("p (h d) -> p h d", d=QK),
+                in1=bias[:, 2 * c : 2 * c + 2, :],
+                op=ALU.add,
+            )
+
+        def products(c, i0):
+            t1 = tmp.tile([P, 2, 2, ROPE], F32, name="t1", tag="t1")
+            t2 = tmp.tile([P, 2, 2, 2, 64], F32, name="t2", tag="t2")
+            nc.vector.tensor_tensor(
+                out=t1[:],
+                in0=res[:, i0 : i0 + 2, 2 * c : 2 * c + 2, 1 + NOPE : HD],
+                in1=c2[:, i0 : i0 + 2].rearrange("p i j e -> p i (j e)").unsqueeze(2).to_broadcast([P, 2, 2, ROPE]),
+                op=ALU.mult,
+            )
+            for e in range(2):
                 nc.vector.tensor_tensor(
-                    out=av[m][:].rearrange("p h j e -> p h (j e)"),
-                    in0=acc[(cc, m)][:].rearrange("p (h d) -> p h d", d=ROPE),
-                    in1=bias[:, 4 * i : 4 * i + 4, NOPE:QK],
-                    op=ALU.add,
-                )
-            for m in ms:
-                nc.vector.tensor_tensor(
-                    out=dst[m],
-                    in0=av[m][:].rearrange("p h j e -> p h (j e)"),
-                    in1=c2[:, m % 2].rearrange("p j e -> p (j e)").unsqueeze(1).to_broadcast([P, 4, ROPE]),
+                    out=t2[:, e],
+                    in0=res[:, i0 : i0 + 2, 2 * c : 2 * c + 2, 1 + NOPE + 1 - e : HD : 2],
+                    in1=sn[:, i0 : i0 + 2, e, :].unsqueeze(2).to_broadcast([P, 2, 2, 64]),
                     op=ALU.mult,
                 )
-            for e in range(2):
-                for m in ms:
-                    nc.vector.tensor_tensor(
-                        out=t2[m][:, e, :, :],
-                        in0=av[m][:, :, :, 1 - e],
-                        in1=sn[:, m % 2, e, :].unsqueeze(1).to_broadcast([P, 4, 64]),
-                        op=ALU.mult,
-                    )
-            for m in ms:
-                d4 = dst[m].rearrange("p h (j e) -> p h j e", e=2)
-                nc.vector.tensor_tensor(out=d4, in0=d4, in1=t2[m][:].rearrange("p e h j -> p h j e"), op=ALU.add)
+            state["prev"] = (c, i0, t1, t2)
 
-        def squares(gq, ms):
-            for m in ms:
-                for h in range(4 * gq, 4 * gq + 4):
-                    junk = tmp.tile([P, QK], F32, name="junk", tag="junk")
-                    nc.scalar.activation(out=junk[:], in_=res[:, m, h, 1:HD], func=ACT.Square, accum_out=ssq[:, m, h : h + 1])
-            for m in ms:
-                nc.scalar.activation(out=res[:, m, 4 * gq : 4 * gq + 4, 0], in_=ssq[:, m, 4 * gq : 4 * gq + 4], func=ACT.Sqrt, bias=1.0)
-                nc.scalar.dma_start(out=o0[P * m : P * (m + 1), 4 * gq : 4 * gq + 4, :], in_=res[:, m, 4 * gq : 4 * gq + 4, :])
+        def rotate_prev(k):
+            if state["prev"] is None:
+                return
+            c, i0, t1, t2 = state["prev"]
+            nc.vector.tensor_tensor(
+                out=res[:, i0 + k, 2 * c : 2 * c + 2, 1 + NOPE : HD].rearrange("p h (j e) -> p h j e", e=2),
+                in0=t1[:, k].rearrange("p h (j e) -> p h j e", e=2),
+                in1=t2[:, :, k].rearrange("p e h j -> p h j e"),
+                op=ALU.add,
+            )
+            if k == 1:
+                state["prev"] = None
+                pending.append((c, i0))
 
-        n_rt = len(row_tiles)
-        n_runs = n_rt // 2
-        for k in range(RAW_BUFS):
-            load(k)
-        pending = {}
-        for s in range(n_runs + 2 + SQ_DELAY):
-            if s < n_runs:
-                for k in (2 * s, 2 * s + 1):
-                    transposes(k)
-                for k in (2 * s, 2 * s + 1):
-                    copies(k)
-                    if k + RAW_BUFS < n_rt:
-                        load(k + RAW_BUFS)
-                if s == 2:
-                    nc.scalar.dma_start(out=biasf[:, 768 : H * QK], in_=wq_b[768 : H * QK].partition_broadcast(P))
-                if s % 2 == 1:
-                    quantize(s // 2 - 1)
-            q = s - 4
-            if 0 <= q < 12:
-                cc = q // 2
-                ms = (2 * (q % 2), 2 * (q % 2) + 1)
-                for m in ms:
-                    matmuls(cc, m)
-                epilogue(cc, ms)
-                if cc in GROUP_DONE:
-                    pending[s + SQ_DELAY] = (GROUP_DONE[cc], ms)
-            if s in pending:
-                squares(pending[s][0], pending[s][1])
+        def sums(n):
+            for rep in range(n):
+                if state["summed"] >= len(pending):
+                    return
+                c, i0 = pending[state["summed"]]
+                state["summed"] = state["summed"] + 1
+                for i in (i0, i0 + 1):
+                    for h in (2 * c, 2 * c + 1):
+                        junk = tmp.tile([P, QK], F32, name="junk", tag="junk")
+                        nc.scalar.activation(out=junk[:], in_=res[:, i, h, 1:HD], func=ACT.Square, accum_out=ssq[:, i, h : h + 1])
+                nc.scalar.activation(
+                    out=res[:, i0 : i0 + 2, 2 * c : 2 * c + 2, 0], in_=ssq[:, i0 : i0 + 2, 2 * c : 2 * c + 2], func=ACT.Sqrt, bias=1.0
+                )
+                lo = (CW + 2) * c // 8 * 8
+                hi = (CW + 2) * (c + 1) // 8 * 8
+                nc.scalar.dma_start(out=o0[:, i0 : i0 + 2, lo:hi], in_=resf[:, i0 : i0 + 2, lo:hi])
+
+        for n in range(RAW_BUFS):
+            load()
+        dummies(WARM)
+        for t in HEAD[0:SORT_AHEAD]:
+            sort_words(t)
+        for n, t in enumerate(HEAD):
+            if n + SORT_AHEAD < len(HEAD):
+                sort_words(HEAD[n + SORT_AHEAD])
+            transposes(t)
+            dummies(HEAD_DUMMIES)
+            copies(t)
+            if n == 0:
+                nc.scalar.dma_start(out=biasf[:, 0 : 2 * CW], in_=wq_b[0 : 2 * CW].partition_broadcast(P))
+                nc.vector.tensor_copy(out=c2[:], in_=cos16[:].unsqueeze(3).to_broadcast([P, NT, 64, 2]))
+            if n == 1:
+                nc.vector.tensor_scalar(out=sn[:, :, 0, :], in0=sin16[:], scalar1=-1.0, scalar2=None, op0=ALU.mult)
+                nc.vector.tensor_copy(out=sn[:, :, 1, :], in_=sin16[:])
+        for c in range(NCH):
+            for i in range(NT):
+                for r in t_plan(c, i):
+                    transposes(("w", r))
+                    copies(("w", r))
+                if i % 2 == 1:
+                    sums(1)
+                if i == 0 and c % 2 == 0 and c < NCH - 2:
+                    lo = (c + 2) * CW
+                    nc.scalar.dma_start(out=biasf[:, lo : lo + 2 * CW], in_=wq_b[lo : lo + 2 * CW].partition_broadcast(P))
+                matmuls(c, i)
+                add_bias(c, i)
+                rotate_prev(i % 2)
+                if i % 2 == 1:
+                    products(c, i - 1)
+        rotate_prev(0)
+        rotate_prev(1)
+        sums(len(pending))
 
         pmax = const.tile([P, 1], F32, name="pmax")
-        nc.vector.tensor_reduce(out=pmax[:], in_=res[:].rearrange("p m h d -> p (m h) d")[:, :, 0], axis=AX.X, op=ALU.max)
+        nc.vector.tensor_reduce(out=pmax[:], in_=res[:].rearrange("p i h d -> p (i h) d")[:, :, 0], axis=AX.X, op=ALU.max)
         spread = ps_t.tile([P, P], F32, name="spread", tag="xt")
         nc.tensor.transpose(spread[:], pmax[:, 0:1].to_broadcast([P, P]), ident[:])
         amax = const.tile([P, 1], F32, name="amax")
@@ -239,17 +304,17 @@ def tile_lorentzmla_pb_kernel(tc, x, freqs_cos, freqs_sin, wq_w, wq_b, out_0, ou
         nc.vector.reciprocal(out=rcp[:], in_=amax[:])
         fac = const.tile([P, 1], F32, name="fac")
         nc.vector.tensor_scalar(out=fac[:], in0=rcp[:], scalar1=448.0, scalar2=None, op0=ALU.mult)
-        resf = res[:].rearrange("p m h d -> p m (h d)")
-        for m in range(4):
+        cuts = (0, 3072, 6176, 9248, NT * ROW)
+        for i in range(NT):
             nc.vector.tensor_scalar(
-                out=res8[:, m, 0:V_SPLIT], in0=resf[:, m, 0:V_SPLIT], scalar1=fac[:, 0:1], scalar2=None, op0=ALU.mult, saturate=False
+                out=res8[:, ROW * i : ROW * i + V_SPLIT], in0=resf[:, i, 0:V_SPLIT], scalar1=fac[:, 0:1], scalar2=None, op0=ALU.mult, saturate=False
             )
             nc.scalar.activation(
-                out=res8[:, m, V_SPLIT : H * HD],
-                in_=resf[:, m, V_SPLIT : H * HD],
+                out=res8[:, ROW * i + V_SPLIT : ROW * (i + 1)],
+                in_=resf[:, i, V_SPLIT:ROW],
                 func=ACT.Identity,
                 scale=fac[:, 0:1],
                 bias=zero1[:, 0:1],
                 saturate=False,
             )
-            nc.sync.dma_start(out=o1[P * m : P * (m + 1), :], in_=res8[:, m, :].bitcast(U8))
+            nc.sync.dma_start(out=o1[:, cuts[i] : cuts[i + 1]], in_=res8[:, cuts[i] : cuts[i + 1]].bitcast(U8))

@@ -7,6 +7,7 @@ F32 = mybir.dt.float32
 BF16 = mybir.dt.bfloat16
 U32 = mybir.dt.uint32
 U8 = mybir.dt.uint8
+I32 = mybir.dt.int32
 FP8X4 = mybir.dt.float8_e4m3fn_x4
 FP8 = mybir.dt.float8_e4m3fn
 ALU = mybir.AluOpType
@@ -32,20 +33,21 @@ CW = 2 * QK
 N_A = 256
 RAW_BUFS = 10
 WARM = 6
-HEAD_DUMMIES = 2
-SORT_AHEAD = 3
+SORT_AHEAD = 2
 V_SPLIT = 2048
 
 HEAD = (("x", 0), ("w", 0), ("w", 1), ("w", 2), ("x", 1), ("x", 2), ("x", 3))
-T_PLAN = ((), (3,), (4,), (5,)), ((6,), (7,), (8,), ())
 
 
 def t_plan(c, i):
-    if c < 2:
-        return T_PLAN[c][i]
-    if c == NCH - 1 or i == 3:
+    if c == NCH - 1:
         return ()
-    return (3 * c + 3 + i,)
+    r = 3 * (c + 1)
+    first = ((r, 0), (r, 1), (r + 1, 0))
+    second = ((r + 1, 1), (r + 2, 0), (r + 2, 1))
+    if c == 0:
+        return ((), first, second, ())[i]
+    return (first, (), second, ())[i]
 
 
 def tile_lorentzmla_pb_kernel(tc, x, freqs_cos, freqs_sin, wq_w, wq_b, out_0, out_1):
@@ -67,14 +69,18 @@ def tile_lorentzmla_pb_kernel(tc, x, freqs_cos, freqs_sin, wq_w, wq_b, out_0, ou
         ps_a = ctx.enter_context(tc.psum_pool(name="ps_a", bufs=4))
         ctx.enter_context(tc.manual_schedule())
 
-        dummy = const.tile([P, TOK], BF16, name="dummy")
-        nc.vector.memset(dummy[:], 0.0)
-        ident = const.tile([P, P], F32, name="ident")
-        make_identity(nc, ident[:])
         one1 = const.tile([P, 1], F32, name="one1")
         nc.vector.memset(one1[:], 1.0)
         zero1 = const.tile([P, 1], F32, name="zero1")
         nc.vector.memset(zero1[:], 0.0)
+        dummy = const.tile([P, TOK], BF16, name="dummy")
+        nc.vector.memset(dummy[:].bitcast(I32), 0)
+        brow = const.tile([P, H * QK], BF16, name="brow")
+        nc.vector.memset(brow[:].bitcast(I32), 0)
+        ones = const.tile([P, P], BF16, name="ones")
+        nc.vector.memset(ones[:], 1.0)
+        ident = const.tile([P, P], F32, name="ident")
+        make_identity(nc, ident[:])
 
         cos16 = const.tile([P, NT, 64], BF16, name="cos16")
         sin16 = const.tile([P, NT, 64], BF16, name="sin16")
@@ -83,6 +89,7 @@ def tile_lorentzmla_pb_kernel(tc, x, freqs_cos, freqs_sin, wq_w, wq_b, out_0, ou
             nc.scalar.dma_start(out=sin16[64 * half : 64 * half + 64], in_=sinv)
         warm = const.tile([P, 1], F32, name="warm")
         nc.scalar.activation(out=warm[:], in_=one1[:], func=ACT.Sqrt)
+        nc.scalar.dma_start(out=brow[0:1, :], in_=wq_b.rearrange("(o n) -> o n", o=1))
         bias = const.tile([P, H, QK], BF16, name="bias")
         biasf = bias[:].rearrange("p h d -> p (h d)")
 
@@ -99,6 +106,7 @@ def tile_lorentzmla_pb_kernel(tc, x, freqs_cos, freqs_sin, wq_w, wq_b, out_0, ou
         order = list(HEAD) + [("w", r) for r in range(3, 3 * NCH)]
         raw = {}
         sorted_tiles = {}
+        spreadb = {}
         banks = {}
         grouped = {}
         codes = {}
@@ -132,22 +140,20 @@ def tile_lorentzmla_pb_kernel(tc, x, freqs_cos, freqs_sin, wq_w, wq_b, out_0, ou
             nc.vector.tensor_copy(out=srt[:], in_=raw[t][:].bitcast(F32).rearrange("p (w u) -> p u w", u=2))
             sorted_tiles[t] = srt
 
-        def transposes(t):
+        def transposes(t, half):
             words = raw[t][:].bitcast(F32)
-            sorted_words = t in sorted_tiles
-            banks[t] = []
-            for half in range(2):
-                xt = ps_t.tile([P, 2, 2, P], F32, name="xt", tag="xt")
-                for a in range(2):
-                    g = 2 * half + a
-                    for u in range(2):
-                        if sorted_words:
-                            src = sorted_tiles[t][:, u, P * g : P * (g + 1)]
-                        else:
-                            src = words[:, 256 * g + u : 256 * (g + 1) : 2]
-                        nc.tensor.transpose(xt[:, a, u, :], src, ident[:])
-                banks[t].append(xt)
-            load()
+            xt = ps_t.tile([P, 2, 2, P], F32, name="xt", tag="xt")
+            for a in range(2):
+                g = 2 * half + a
+                for u in range(2):
+                    if t in sorted_tiles:
+                        src = sorted_tiles[t][:, u, P * g : P * (g + 1)]
+                    else:
+                        src = words[:, 256 * g + u : 256 * (g + 1) : 2]
+                    nc.tensor.transpose(xt[:, a, u, :], src, ident[:])
+            banks[(t, half)] = xt
+            if half == 1:
+                load()
 
         def quantize_x(i):
             nc.vector.quantize_mx(
@@ -166,24 +172,31 @@ def tile_lorentzmla_pb_kernel(tc, x, freqs_cos, freqs_sin, wq_w, wq_b, out_0, ou
             for lo, hi in ((0, 1024), (1024, PASSES * CW)):
                 nc.vector.quantize_mx(out=cf[:, lo:hi].bitcast(FP8X4), scales=sf[:, lo:hi], in_=gin[:, 4 * lo : 4 * hi])
 
-        def copies(t):
+        def copies(t, half):
             kind, r = t
             if kind == "x":
                 key, col = ("x", r), 0
-                grouped[key] = gwp.tile([P, PASSES, P, 4], BF16, name="gx", tag="gx", align_bytes=64)
+                if half == 0:
+                    grouped[key] = gwp.tile([P, PASSES, P, 4], BF16, name="gx", tag="gx", align_bytes=64)
             else:
                 key, col = ("w", r // 3), P * (r % 3)
-                if r % 3 == 0:
+                if r % 3 == 0 and half == 0:
                     grouped[key] = gwp.tile([P, PASSES, CW, 4], BF16, name="gw", tag="gw", align_bytes=64)
-            for half in range(2):
-                nc.scalar.copy(
-                    out=grouped[key][:, 2 * half : 2 * half + 2, col : col + P, :].bitcast(F32),
-                    in_=banks[t][half][:].rearrange("p a u r -> p a r u"),
-                )
-            if kind == "x":
+            nc.scalar.copy(
+                out=grouped[key][:, 2 * half : 2 * half + 2, col : col + P, :].bitcast(F32),
+                in_=banks[(t, half)][:].rearrange("p a u r -> p a r u"),
+            )
+            if half == 1 and kind == "x":
                 quantize_x(r)
-            elif r % 3 == 2:
+            elif half == 1 and r % 3 == 2:
                 quantize_w(r // 3)
+
+        def bias_matmul(q):
+            if q % 2 == 0:
+                spreadb[q // 2] = ps_a.tile([P, 2 * TOK], BF16, name="pb", tag="acc")
+            nc.tensor.matmul(
+                out=spreadb[q // 2][:, TOK * (q % 2) : TOK * (q % 2 + 1)], lhsT=ones[:], rhs=brow[:, TOK * q : TOK * (q + 1)], start=True, stop=True
+            )
 
         def matmuls(c, i):
             wc, ws = codes[c]
@@ -266,25 +279,30 @@ def tile_lorentzmla_pb_kernel(tc, x, freqs_cos, freqs_sin, wq_w, wq_b, out_0, ou
         for n, t in enumerate(HEAD):
             if n + SORT_AHEAD < len(HEAD):
                 sort_words(HEAD[n + SORT_AHEAD])
-            transposes(t)
-            dummies(HEAD_DUMMIES)
-            copies(t)
+            transposes(t, 0)
+            transposes(t, 1)
             if n == 0:
-                nc.scalar.dma_start(out=biasf[:, 0 : 2 * CW], in_=wq_b[0 : 2 * CW].partition_broadcast(P))
+                dummies(1)
+            else:
+                bias_matmul(n - 1)
+            copies(t, 0)
+            copies(t, 1)
+            if n == 4:
+                nc.vector.tensor_copy(out=biasf[:, 0 : 2 * TOK], in_=spreadb[0][:])
                 nc.vector.tensor_copy(out=c2[:], in_=cos16[:].unsqueeze(3).to_broadcast([P, NT, 64, 2]))
-            if n == 1:
+            if n == 5:
                 nc.vector.tensor_scalar(out=sn[:, :, 0, :], in0=sin16[:], scalar1=-1.0, scalar2=None, op0=ALU.mult)
                 nc.vector.tensor_copy(out=sn[:, :, 1, :], in_=sin16[:])
+        for k in (1, 2):
+            nc.scalar.copy(out=biasf[:, 2 * TOK * k : 2 * TOK * (k + 1)], in_=spreadb[k][:])
         for c in range(NCH):
             for i in range(NT):
-                for r in t_plan(c, i):
-                    transposes(("w", r))
-                    copies(("w", r))
-                if i % 2 == 1:
+                for r, half in t_plan(c, i):
+                    transposes(("w", r), half)
+                for r, half in t_plan(c, i):
+                    copies(("w", r), half)
+                if len(t_plan(c, i)) > 0 or c == NCH - 1:
                     sums(1)
-                if i == 0 and c % 2 == 0 and c < NCH - 2:
-                    lo = (c + 2) * CW
-                    nc.scalar.dma_start(out=biasf[:, lo : lo + 2 * CW], in_=wq_b[lo : lo + 2 * CW].partition_broadcast(P))
                 matmuls(c, i)
                 add_bias(c, i)
                 rotate_prev(i % 2)

@@ -269,7 +269,7 @@ def tile_lorentzmla_pb_kernel(tc, x, freqs_cos, freqs_sin, wq_w, wq_b, out_0, ou
                 )
                 lo = (CW + 2) * c // 8 * 8
                 hi = (CW + 2) * (c + 1) // 8 * 8
-                nc.scalar.dma_start(out=o0[:, i0 : i0 + 2, lo:hi], in_=resf[:, i0 : i0 + 2, lo:hi])
+                nc.sync.dma_start(out=o0[:, i0 : i0 + 2, lo:hi], in_=resf[:, i0 : i0 + 2, lo:hi])
 
         for n in range(RAW_BUFS):
             load()

@@ -34,9 +34,10 @@ N_A = 256
 RAW_BUFS = 10
 WARM = 6
 SORT_AHEAD = 2
+N_SORTED = 4
 V_SPLIT = 2048
 
-HEAD = (("x", 0), ("w", 0), ("w", 1), ("w", 2), ("x", 1), ("x", 2), ("x", 3))
+HEAD = (("w", 0), ("w", 1), ("w", 2), ("x", 0), ("x", 1), ("x", 2), ("x", 3))
 
 
 def t_plan(c, i):
@@ -123,8 +124,8 @@ def tile_lorentzmla_pb_kernel(tc, x, freqs_cos, freqs_sin, wq_w, wq_b, out_0, ou
             t = rawp.tile([P, K], BF16, name="raw", tag="raw")
             raw[(kind, r)] = t
             if n == 0:
-                nc.sync.dma_start(out=t[:, 0 : K // 2], in_=xv[:, r, 0 : K // 2])
-                nc.sync.dma_start(out=t[:, K // 2 : K], in_=xv[:, r, K // 2 : K])
+                nc.sync.dma_start(out=t[:, 0 : K // 2], in_=wq_w[0:P, 0 : K // 2])
+                nc.sync.dma_start(out=t[:, K // 2 : K], in_=wq_w[0:P, K // 2 : K])
             elif kind == "x":
                 nc.sync.dma_start(out=t[:], in_=xv[:, r, :])
             else:
@@ -269,7 +270,8 @@ def tile_lorentzmla_pb_kernel(tc, x, freqs_cos, freqs_sin, wq_w, wq_b, out_0, ou
                 )
                 lo = (CW + 2) * c // 8 * 8
                 hi = (CW + 2) * (c + 1) // 8 * 8
-                nc.sync.dma_start(out=o0[:, i0 : i0 + 2, lo:hi], in_=resf[:, i0 : i0 + 2, lo:hi])
+                for i in (i0, i0 + 1):
+                    nc.sync.dma_start(out=o0[:, i, lo:hi], in_=resf[:, i, lo:hi])
 
         for n in range(RAW_BUFS):
             load()
@@ -277,7 +279,7 @@ def tile_lorentzmla_pb_kernel(tc, x, freqs_cos, freqs_sin, wq_w, wq_b, out_0, ou
         for t in HEAD[0:SORT_AHEAD]:
             sort_words(t)
         for n, t in enumerate(HEAD):
-            if n + SORT_AHEAD < len(HEAD):
+            if n + SORT_AHEAD < N_SORTED:
                 sort_words(HEAD[n + SORT_AHEAD])
             transposes(t, 0)
             transposes(t, 1)
@@ -301,13 +303,14 @@ def tile_lorentzmla_pb_kernel(tc, x, freqs_cos, freqs_sin, wq_w, wq_b, out_0, ou
                     transposes(("w", r), half)
                 for r, half in t_plan(c, i):
                     copies(("w", r), half)
-                if len(t_plan(c, i)) > 0 or c == NCH - 1:
-                    sums(1)
+                n_ready = len(pending)
                 matmuls(c, i)
                 add_bias(c, i)
                 rotate_prev(i % 2)
                 if i % 2 == 1:
                     products(c, i - 1)
+                if (len(t_plan(c, i)) > 0 or c == NCH - 1) and state["summed"] < n_ready:
+                    sums(1)
         rotate_prev(0)
         rotate_prev(1)
         sums(len(pending))

@@ -66,8 +66,10 @@ def tile_lorentzmla_pb_kernel(tc, x, freqs_cos, freqs_sin, wq_w, wq_b, out_0, ou
         gwp = ctx.enter_context(tc.tile_pool(name="gwp", bufs=2))
         cdp = ctx.enter_context(tc.tile_pool(name="cdp", bufs=3))
         tmp = ctx.enter_context(tc.tile_pool(name="tmp", bufs=3))
-        ps_t = ctx.enter_context(tc.psum_pool(name="ps_t", bufs=4))
+        abp = ctx.enter_context(tc.tile_pool(name="abp", bufs=2))
+        ps_t = ctx.enter_context(tc.psum_pool(name="ps_t", bufs=3))
         ps_a = ctx.enter_context(tc.psum_pool(name="ps_a", bufs=4))
+        ps_c = ctx.enter_context(tc.psum_pool(name="ps_c", bufs=1))
         ctx.enter_context(tc.manual_schedule())
 
         one1 = const.tile([P, 1], F32, name="one1")
@@ -82,6 +84,11 @@ def tile_lorentzmla_pb_kernel(tc, x, freqs_cos, freqs_sin, wq_w, wq_b, out_0, ou
         nc.vector.memset(ones[:], 1.0)
         ident = const.tile([P, P], F32, name="ident")
         make_identity(nc, ident[:])
+        ident16 = const.tile([P, P], BF16, name="ident16")
+        make_identity(nc, ident16[:])
+        u2 = [const.tile([P, 2, 2, QK], F32, name="u2_%d" % n) for n in range(2)]
+        for n in range(2):
+            nc.gpsimd.memset(u2[n][:], 0.0)
 
         cos16 = const.tile([P, NT, 64], BF16, name="cos16")
         sin16 = const.tile([P, NT, 64], BF16, name="sin16")
@@ -94,8 +101,9 @@ def tile_lorentzmla_pb_kernel(tc, x, freqs_cos, freqs_sin, wq_w, wq_b, out_0, ou
         bias = const.tile([P, H, QK], BF16, name="bias")
         biasf = bias[:].rearrange("p h d -> p (h d)")
 
-        c2 = const.tile([P, NT, 64, 2], F32, name="c2")
-        sn = const.tile([P, NT, 2, 64], F32, name="sn")
+        c2 = const.tile([P, NT, 64, 2], BF16, name="c2")
+        sn = const.tile([P, NT, 64, 2], BF16, name="sn")
+        tab = ps_c.tile([P, 2, NT, ROPE], BF16, name="tab")
 
         res = const.tile([P, NT, H, HD], F32, name="res")
         resf = res[:].rearrange("p i h d -> p i (h d)")
@@ -112,8 +120,8 @@ def tile_lorentzmla_pb_kernel(tc, x, freqs_cos, freqs_sin, wq_w, wq_b, out_0, ou
         grouped = {}
         codes = {}
         acc = {}
-        state = {"loaded": 0, "prev": None, "summed": 0}
-        pending = []
+        ab = {}
+        state = {"loaded": 0}
 
         def load():
             n = state["loaded"]
@@ -216,51 +224,35 @@ def tile_lorentzmla_pb_kernel(tc, x, freqs_cos, freqs_sin, wq_w, wq_b, out_0, ou
                     )
 
         def add_bias(c, i):
+            if i % 2 == 0:
+                ab[(c, i // 2)] = abp.tile([P, 2, 2, QK], F32, name="ab", tag="ab")
             nc.vector.tensor_tensor(
-                out=res[:, i, 2 * c : 2 * c + 2, 1:HD],
+                out=ab[(c, i // 2)][:, i % 2],
                 in0=acc[(c, i)][:].rearrange("p (h d) -> p h d", d=QK),
                 in1=bias[:, 2 * c : 2 * c + 2, :],
                 op=ALU.add,
             )
 
-        def products(c, i0):
-            t1 = tmp.tile([P, 2, 2, ROPE], F32, name="t1", tag="t1")
-            t2 = tmp.tile([P, 2, 2, 2, 64], F32, name="t2", tag="t2")
+        def rope(c, k, adder):
+            a = ab[(c, k)]
+            u = u2[k]
             nc.vector.tensor_tensor(
-                out=t1[:],
-                in0=res[:, i0 : i0 + 2, 2 * c : 2 * c + 2, 1 + NOPE : HD],
-                in1=c2[:, i0 : i0 + 2].rearrange("p i j e -> p i (j e)").unsqueeze(2).to_broadcast([P, 2, 2, ROPE]),
+                out=u[:, :, :, NOPE:QK].rearrange("p k h (j e) -> p k h j e", e=2),
+                in0=a[:, :, :, NOPE:QK].rearrange("p k h (j e) -> p k h j e", e=2)[:, :, :, :, ::-1],
+                in1=tab[:, 1, 2 * k : 2 * k + 2].rearrange("p i (j e) -> p i j e", e=2).unsqueeze(2).to_broadcast([P, 2, 2, 64, 2]),
                 op=ALU.mult,
             )
-            for e in range(2):
-                nc.vector.tensor_tensor(
-                    out=t2[:, e],
-                    in0=res[:, i0 : i0 + 2, 2 * c : 2 * c + 2, 1 + NOPE + 1 - e : HD : 2],
-                    in1=sn[:, i0 : i0 + 2, e, :].unsqueeze(2).to_broadcast([P, 2, 2, 64]),
-                    op=ALU.mult,
-                )
-            state["prev"] = (c, i0, t1, t2)
-
-        def rotate_prev(k):
-            if state["prev"] is None:
-                return
-            c, i0, t1, t2 = state["prev"]
             nc.vector.tensor_tensor(
-                out=res[:, i0 + k, 2 * c : 2 * c + 2, 1 + NOPE : HD].rearrange("p h (j e) -> p h j e", e=2),
-                in0=t1[:, k].rearrange("p h (j e) -> p h j e", e=2),
-                in1=t2[:, :, k].rearrange("p e h j -> p h j e"),
-                op=ALU.add,
+                out=a[:, :, :, NOPE:QK],
+                in0=a[:, :, :, NOPE:QK],
+                in1=tab[:, 0, 2 * k : 2 * k + 2].unsqueeze(2).to_broadcast([P, 2, 2, ROPE]),
+                op=ALU.mult,
             )
-            if k == 1:
-                state["prev"] = None
-                pending.append((c, i0))
+            for n in range(2):
+                adder.tensor_tensor(out=res[:, 2 * k + n, 2 * c : 2 * c + 2, 1:HD], in0=a[:, n], in1=u[:, n], op=ALU.add)
 
-        def sums(n):
-            for rep in range(n):
-                if state["summed"] >= len(pending):
-                    return
-                c, i0 = pending[state["summed"]]
-                state["summed"] = state["summed"] + 1
+        def sums(c, i0):
+            if c >= 0:
                 for i in (i0, i0 + 1):
                     for h in (2 * c, 2 * c + 1):
                         junk = tmp.tile([P, QK], F32, name="junk", tag="junk")
@@ -293,8 +285,12 @@ def tile_lorentzmla_pb_kernel(tc, x, freqs_cos, freqs_sin, wq_w, wq_b, out_0, ou
                 nc.vector.tensor_copy(out=biasf[:, 0 : 2 * TOK], in_=spreadb[0][:])
                 nc.vector.tensor_copy(out=c2[:], in_=cos16[:].unsqueeze(3).to_broadcast([P, NT, 64, 2]))
             if n == 5:
-                nc.vector.tensor_scalar(out=sn[:, :, 0, :], in0=sin16[:], scalar1=-1.0, scalar2=None, op0=ALU.mult)
-                nc.vector.tensor_copy(out=sn[:, :, 1, :], in_=sin16[:])
+                nc.vector.tensor_scalar(out=sn[:, :, :, 0], in0=sin16[:], scalar1=-1.0, scalar2=None, op0=ALU.mult)
+                nc.vector.tensor_copy(out=sn[:, :, :, 1], in_=sin16[:])
+        for n, t in enumerate((c2, sn)):
+            nc.tensor.matmul(
+                out=tab[:, n].rearrange("p i d -> p (i d)"), lhsT=ident16[:], rhs=t[:].rearrange("p i j e -> p (i j e)"), start=True, stop=True
+            )
         for k in (1, 2):
             nc.scalar.copy(out=biasf[:, 2 * TOK * k : 2 * TOK * (k + 1)], in_=spreadb[k][:])
         for c in range(NCH):
@@ -303,17 +299,14 @@ def tile_lorentzmla_pb_kernel(tc, x, freqs_cos, freqs_sin, wq_w, wq_b, out_0, ou
                     transposes(("w", r), half)
                 for r, half in t_plan(c, i):
                     copies(("w", r), half)
-                n_ready = len(pending)
                 matmuls(c, i)
                 add_bias(c, i)
-                rotate_prev(i % 2)
                 if i % 2 == 1:
-                    products(c, i - 1)
-                if (len(t_plan(c, i)) > 0 or c == NCH - 1) and state["summed"] < n_ready:
-                    sums(1)
-        rotate_prev(0)
-        rotate_prev(1)
-        sums(len(pending))
+                    rope(c, i // 2, nc.vector if (c == NCH - 1 and i == NT - 1) else nc.gpsimd)
+                else:
+                    sums(c - 1, i)
+        sums(NCH - 1, 0)
+        sums(NCH - 1, 2)
 
         pmax = const.tile([P, 1], F32, name="pmax")
         nc.vector.tensor_reduce(out=pmax[:], in_=res[:].rearrange("p i h d -> p (i h) d")[:, :, 0], axis=AX.X, op=ALU.max)

@@ -31,6 +31,7 @@ FLOPS = 2 * TOK * H * QK * K
 NCH = 8
 CW = 2 * QK
 N_A = 256
+WIDTHS = (N_A, CW - N_A)
 RAW_BUFS = 10
 WARM = 6
 SORT_AHEAD = 2
@@ -86,24 +87,26 @@ def tile_lorentzmla_pb_kernel(tc, x, freqs_cos, freqs_sin, wq_w, wq_b, out_0, ou
         make_identity(nc, ident[:])
         ident16 = const.tile([P, P], BF16, name="ident16")
         make_identity(nc, ident16[:])
+        minus16 = const.tile([P, P], BF16, name="minus16")
+        nc.gpsimd.tensor_scalar(out=minus16[:], in0=ident16[:], scalar1=-1.0, scalar2=0.0, op0=ALU.mult, op1=ALU.add)
         u2 = [const.tile([P, 2, 2, QK], F32, name="u2_%d" % n) for n in range(2)]
-        for n in range(2):
-            nc.gpsimd.memset(u2[n][:], 0.0)
 
         cos16 = const.tile([P, NT, 64], BF16, name="cos16")
-        sin16 = const.tile([P, NT, 64], BF16, name="sin16")
+        zsz = const.tile([P, 3, NT * 64], BF16, name="zsz")
+        nc.vector.memset(zsz[:, 0, :].bitcast(I32), 0)
+        nc.vector.memset(zsz[:, 2, :].bitcast(I32), 0)
         for half in range(2):
             nc.scalar.dma_start(out=cos16[64 * half : 64 * half + 64], in_=cosv)
-            nc.scalar.dma_start(out=sin16[64 * half : 64 * half + 64], in_=sinv)
+            nc.scalar.dma_start(out=zsz[64 * half : 64 * half + 64, 1, :].rearrange("p (i j) -> p i j", i=NT), in_=sinv)
         warm = const.tile([P, 1], F32, name="warm")
         nc.scalar.activation(out=warm[:], in_=one1[:], func=ACT.Sqrt)
         nc.scalar.dma_start(out=brow[0:1, :], in_=wq_b.rearrange("(o n) -> o n", o=1))
         bias = const.tile([P, H, QK], BF16, name="bias")
         biasf = bias[:].rearrange("p h d -> p (h d)")
 
-        c2 = const.tile([P, NT, 64, 2], BF16, name="c2")
-        sn = const.tile([P, NT, 64, 2], BF16, name="sn")
         tab = ps_c.tile([P, 2, NT, ROPE], BF16, name="tab")
+        for n in range(2):
+            nc.gpsimd.memset(u2[n][:], 0.0)
 
         res = const.tile([P, NT, H, HD], F32, name="res")
         resf = res[:].rearrange("p i h d -> p i (h d)")
@@ -171,15 +174,16 @@ def tile_lorentzmla_pb_kernel(tc, x, freqs_cos, freqs_sin, wq_w, wq_b, out_0, ou
                 in_=grouped[("x", i)][:].rearrange("p g n t -> p (g n t)"),
             )
 
-        def quantize_w(c):
-            wc = cdp.tile([P, PASSES, CW], U32, name="w_codes", tag="w_codes", align_bytes=64)
-            ws = cdp.tile([P, PASSES, CW], U8, name="w_scales", tag="w_scales", align_bytes=64)
-            codes[c] = (wc, ws)
-            gin = grouped[("w", c)][:].rearrange("p g n t -> p (g n t)")
-            cf = wc[:].rearrange("p g n -> p (g n)")
-            sf = ws[:].rearrange("p g n -> p (g n)")
-            for lo, hi in ((0, 1024), (1024, PASSES * CW)):
-                nc.vector.quantize_mx(out=cf[:, lo:hi].bitcast(FP8X4), scales=sf[:, lo:hi], in_=gin[:, 4 * lo : 4 * hi])
+        def quantize_w(c, part):
+            width = WIDTHS[part]
+            wc = cdp.tile([P, PASSES, width], U32, name="w_codes%d" % part, tag="w_codes%d" % part, align_bytes=64)
+            ws = cdp.tile([P, PASSES, width], U8, name="w_scales%d" % part, tag="w_scales%d" % part, align_bytes=64)
+            codes[(c, part)] = (wc, ws)
+            nc.vector.quantize_mx(
+                out=wc[:].rearrange("p g n -> p (g n)").bitcast(FP8X4),
+                scales=ws[:].rearrange("p g n -> p (g n)"),
+                in_=grouped[("w", c, part)][:].rearrange("p g n t -> p (g n t)"),
+            )
 
         def copies(t, half):
             kind, r = t
@@ -188,17 +192,18 @@ def tile_lorentzmla_pb_kernel(tc, x, freqs_cos, freqs_sin, wq_w, wq_b, out_0, ou
                 if half == 0:
                     grouped[key] = gwp.tile([P, PASSES, P, 4], BF16, name="gx", tag="gx", align_bytes=64)
             else:
-                key, col = ("w", r // 3), P * (r % 3)
-                if r % 3 == 0 and half == 0:
-                    grouped[key] = gwp.tile([P, PASSES, CW, 4], BF16, name="gw", tag="gw", align_bytes=64)
+                part = r % 3 // 2
+                key, col = ("w", r // 3, part), P * (r % 3 % 2)
+                if col == 0 and half == 0:
+                    grouped[key] = gwp.tile([P, PASSES, WIDTHS[part], 4], BF16, name="gw%d" % part, tag="gw%d" % part, align_bytes=64)
             nc.scalar.copy(
                 out=grouped[key][:, 2 * half : 2 * half + 2, col : col + P, :].bitcast(F32),
                 in_=banks[(t, half)][:].rearrange("p a u r -> p a r u"),
             )
             if half == 1 and kind == "x":
                 quantize_x(r)
-            elif half == 1 and r % 3 == 2:
-                quantize_w(r // 3)
+            elif half == 1 and r % 3 >= 1:
+                quantize_w(r // 3, r % 3 - 1)
 
         def bias_matmul(q):
             if q % 2 == 0:
@@ -207,18 +212,36 @@ def tile_lorentzmla_pb_kernel(tc, x, freqs_cos, freqs_sin, wq_w, wq_b, out_0, ou
                 out=spreadb[q // 2][:, TOK * (q % 2) : TOK * (q % 2 + 1)], lhsT=ones[:], rhs=brow[:, TOK * q : TOK * (q + 1)], start=True, stop=True
             )
 
+        def table_matmul(n):
+            if n == 0:
+                nc.tensor.matmul(
+                    out=tab[:, 0].rearrange("p i (j e) -> p (i j) e", e=2),
+                    lhsT=ident16[:],
+                    rhs=cos16[:].rearrange("p i j -> p (i j)").unsqueeze(2).to_broadcast([P, NT * 64, 2]),
+                    start=True,
+                    stop=True,
+                )
+            else:
+                nc.tensor.matmul(
+                    out=tab[:, 1].rearrange("p i (j e) -> p (i j) e", e=2),
+                    lhsT=(ident16, minus16)[n - 1][:],
+                    rhs=zsz[:, n - 1 : n + 1, :].rearrange("p e n -> p n e"),
+                    start=(n == 1),
+                    stop=(n == 2),
+                )
+
         def matmuls(c, i):
-            wc, ws = codes[c]
             a = ps_a.tile([P, CW], F32, name="acc", tag="acc")
             acc[(c, i)] = a
-            for lo, hi in ((0, N_A), (N_A, CW)):
+            for part in range(2):
+                wc, ws = codes[(c, part)]
                 for g in range(PASSES):
                     nc.tensor.matmul_mx(
-                        out=a[:, lo:hi],
+                        out=a[:, N_A * part : N_A * part + WIDTHS[part]],
                         lhsT=x_codes[:, i, g, :].bitcast(FP8X4),
                         lhsT_scale=x_scales[:, i, g, :],
-                        rhs=wc[:, g, lo:hi].bitcast(FP8X4),
-                        rhs_scale=ws[:, g, lo:hi],
+                        rhs=wc[:, g, :].bitcast(FP8X4),
+                        rhs_scale=ws[:, g, :],
                         start=(g == 0),
                         stop=(g == PASSES - 1),
                     )
@@ -279,18 +302,12 @@ def tile_lorentzmla_pb_kernel(tc, x, freqs_cos, freqs_sin, wq_w, wq_b, out_0, ou
                 dummies(1)
             else:
                 bias_matmul(n - 1)
+            if 1 <= n <= 3:
+                table_matmul(n - 1)
             copies(t, 0)
             copies(t, 1)
             if n == 4:
                 nc.vector.tensor_copy(out=biasf[:, 0 : 2 * TOK], in_=spreadb[0][:])
-                nc.vector.tensor_copy(out=c2[:], in_=cos16[:].unsqueeze(3).to_broadcast([P, NT, 64, 2]))
-            if n == 5:
-                nc.vector.tensor_scalar(out=sn[:, :, :, 0], in0=sin16[:], scalar1=-1.0, scalar2=None, op0=ALU.mult)
-                nc.vector.tensor_copy(out=sn[:, :, :, 1], in_=sin16[:])
-        for n, t in enumerate((c2, sn)):
-            nc.tensor.matmul(
-                out=tab[:, n].rearrange("p i d -> p (i d)"), lhsT=ident16[:], rhs=t[:].rearrange("p i j e -> p (i j e)"), start=True, stop=True
-            )
         for k in (1, 2):
             nc.scalar.copy(out=biasf[:, 2 * TOK * k : 2 * TOK * (k + 1)], in_=spreadb[k][:])
         for c in range(NCH):

@@ -42,14 +42,19 @@ HEAD = (("w", 0), ("w", 1), ("w", 2), ("x", 0), ("x", 1), ("x", 2), ("x", 3))
 
 
 def t_plan(c, i):
-    if c == NCH - 1:
+    slot = NT * c + i
+    if 1 <= slot <= 3:
+        n = slot - 1
+    elif slot >= 4 and slot % 2 == 0:
+        n = slot // 2 + 1
+    else:
         return ()
-    r = 3 * (c + 1)
-    first = ((r, 0), (r, 1), (r + 1, 0))
-    second = ((r + 1, 1), (r + 2, 0), (r + 2, 1))
-    if c == 0:
-        return ((), first, second, ())[i]
-    return (first, (), second, ())[i]
+    if n >= 2 * (NCH - 1):
+        return ()
+    r = 3 * (1 + n // 2)
+    if n % 2 == 0:
+        return ((r, 0), (r, 1), (r + 1, 0))
+    return ((r + 1, 1), (r + 2, 0), (r + 2, 1))
 
 
 def tile_lorentzmla_pb_kernel(tc, x, freqs_cos, freqs_sin, wq_w, wq_b, out_0, out_1):
@@ -67,7 +72,7 @@ def tile_lorentzmla_pb_kernel(tc, x, freqs_cos, freqs_sin, wq_w, wq_b, out_0, ou
         gwp = ctx.enter_context(tc.tile_pool(name="gwp", bufs=2))
         cdp = ctx.enter_context(tc.tile_pool(name="cdp", bufs=3))
         tmp = ctx.enter_context(tc.tile_pool(name="tmp", bufs=3))
-        abp = ctx.enter_context(tc.tile_pool(name="abp", bufs=2))
+        abp = ctx.enter_context(tc.tile_pool(name="abp", bufs=3))
         ps_t = ctx.enter_context(tc.psum_pool(name="ps_t", bufs=3))
         ps_a = ctx.enter_context(tc.psum_pool(name="ps_a", bufs=4))
         ps_c = ctx.enter_context(tc.psum_pool(name="ps_c", bufs=1))
@@ -124,7 +129,8 @@ def tile_lorentzmla_pb_kernel(tc, x, freqs_cos, freqs_sin, wq_w, wq_b, out_0, ou
         codes = {}
         acc = {}
         ab = {}
-        state = {"loaded": 0}
+        state = {"loaded": 0, "summed": 0, "slot": 0}
+        added = []
 
         def load():
             n = state["loaded"]
@@ -256,15 +262,16 @@ def tile_lorentzmla_pb_kernel(tc, x, freqs_cos, freqs_sin, wq_w, wq_b, out_0, ou
                 op=ALU.add,
             )
 
-        def rope(c, k, adder):
-            a = ab[(c, k)]
-            u = u2[k]
+        def rope_sin(c, k):
             nc.vector.tensor_tensor(
-                out=u[:, :, :, NOPE:QK].rearrange("p k h (j e) -> p k h j e", e=2),
-                in0=a[:, :, :, NOPE:QK].rearrange("p k h (j e) -> p k h j e", e=2)[:, :, :, :, ::-1],
+                out=u2[k][:, :, :, NOPE:QK].rearrange("p k h (j e) -> p k h j e", e=2),
+                in0=ab[(c, k)][:, :, :, NOPE:QK].rearrange("p k h (j e) -> p k h j e", e=2)[:, :, :, :, ::-1],
                 in1=tab[:, 1, 2 * k : 2 * k + 2].rearrange("p i (j e) -> p i j e", e=2).unsqueeze(2).to_broadcast([P, 2, 2, 64, 2]),
                 op=ALU.mult,
             )
+
+        def rope_cos(c, k, adder):
+            a = ab[(c, k)]
             nc.vector.tensor_tensor(
                 out=a[:, :, :, NOPE:QK],
                 in0=a[:, :, :, NOPE:QK],
@@ -272,10 +279,12 @@ def tile_lorentzmla_pb_kernel(tc, x, freqs_cos, freqs_sin, wq_w, wq_b, out_0, ou
                 op=ALU.mult,
             )
             for n in range(2):
-                adder.tensor_tensor(out=res[:, 2 * k + n, 2 * c : 2 * c + 2, 1:HD], in0=a[:, n], in1=u[:, n], op=ALU.add)
+                adder.tensor_tensor(out=res[:, 2 * k + n, 2 * c : 2 * c + 2, 1:HD], in0=a[:, n], in1=u2[k][:, n], op=ALU.add)
+            added.append((c, 2 * k, state["slot"]))
 
-        def sums(c, i0):
-            if c >= 0:
+        def sums(n):
+            for c, i0, slot in added[state["summed"] : state["summed"] + n]:
+                state["summed"] = state["summed"] + 1
                 for i in (i0, i0 + 1):
                     for h in (2 * c, 2 * c + 1):
                         junk = tmp.tile([P, QK], F32, name="junk", tag="junk")
@@ -316,14 +325,25 @@ def tile_lorentzmla_pb_kernel(tc, x, freqs_cos, freqs_sin, wq_w, wq_b, out_0, ou
                     transposes(("w", r), half)
                 for r, half in t_plan(c, i):
                     copies(("w", r), half)
+                state["slot"] = NT * c + i
                 matmuls(c, i)
                 add_bias(c, i)
-                if i % 2 == 1:
-                    rope(c, i // 2, nc.vector if (c == NCH - 1 and i == NT - 1) else nc.gpsimd)
-                else:
-                    sums(c - 1, i)
-        sums(NCH - 1, 0)
-        sums(NCH - 1, 2)
+                if i == 0 and c > 0:
+                    rope_sin(c - 1, 1)
+                if i == 1 and c > 0:
+                    rope_cos(c - 1, 1, nc.gpsimd)
+                if i == 2:
+                    rope_sin(c, 0)
+                if i == 3:
+                    rope_cos(c, 0, nc.gpsimd)
+                    if c + 3 < NCH:
+                        sort_words(("w", 3 * (c + 3)))
+                lag = 1 if c == NCH - 1 else 2
+                if (i % 2 == 0 or c == NCH - 1) and state["summed"] < len(added) and added[state["summed"]][2] + lag <= NT * c + i:
+                    sums(1)
+        rope_sin(NCH - 1, 1)
+        rope_cos(NCH - 1, 1, nc.vector)
+        sums(len(added))
 
         pmax = const.tile([P, 1], F32, name="pmax")
         nc.vector.tensor_reduce(out=pmax[:], in_=res[:].rearrange("p i h d -> p (i h) d")[:, :, 0], axis=AX.X, op=ALU.max)

@@ -36,7 +36,7 @@ RAW_BUFS = 10
 WARM = 6
 SORT_AHEAD = 2
 N_SORTED = 4
-V_SPLIT = 2048
+CUTS = (0, 3584, 7168, 10240, 11776, NT * ROW)
 
 HEAD = (("w", 0), ("w", 1), ("w", 2), ("x", 0), ("x", 1), ("x", 2), ("x", 3))
 
@@ -278,8 +278,7 @@ def tile_lorentzmla_pb_kernel(tc, x, freqs_cos, freqs_sin, wq_w, wq_b, out_0, ou
                 in1=tab[:, 0, 2 * k : 2 * k + 2].unsqueeze(2).to_broadcast([P, 2, 2, ROPE]),
                 op=ALU.mult,
             )
-            for n in range(2):
-                adder.tensor_tensor(out=res[:, 2 * k + n, 2 * c : 2 * c + 2, 1:HD], in0=a[:, n], in1=u2[k][:, n], op=ALU.add)
+            adder.tensor_tensor(out=res[:, 2 * k : 2 * k + 2, 2 * c : 2 * c + 2, 1:HD], in0=a[:], in1=u2[k][:], op=ALU.add)
             added.append((c, 2 * k, state["slot"]))
 
         def sums(n):
@@ -349,23 +348,14 @@ def tile_lorentzmla_pb_kernel(tc, x, freqs_cos, freqs_sin, wq_w, wq_b, out_0, ou
         nc.vector.tensor_reduce(out=pmax[:], in_=res[:].rearrange("p i h d -> p (i h) d")[:, :, 0], axis=AX.X, op=ALU.max)
         spread = ps_t.tile([P, P], F32, name="spread", tag="xt")
         nc.tensor.transpose(spread[:], pmax[:, 0:1].to_broadcast([P, P]), ident[:])
-        amax = const.tile([P, 1], F32, name="amax")
-        nc.vector.tensor_reduce(out=amax[:], in_=spread[:], axis=AX.X, op=ALU.max)
-        rcp = const.tile([P, 1], F32, name="rcp")
-        nc.vector.reciprocal(out=rcp[:], in_=amax[:])
+        scaled = const.tile([P, P], F32, name="scaled")
+        s448 = const.tile([P, 1], F32, name="s448")
+        nc.vector.tensor_scalar(out=scaled[:], in0=spread[:], scalar1=1.0 / 448.0, scalar2=None, op0=ALU.mult, op1=ALU.max, accum_out=s448[:])
         fac = const.tile([P, 1], F32, name="fac")
-        nc.vector.tensor_scalar(out=fac[:], in0=rcp[:], scalar1=448.0, scalar2=None, op0=ALU.mult)
-        cuts = (0, 3072, 6176, 9248, NT * ROW)
-        for i in range(NT):
-            nc.vector.tensor_scalar(
-                out=res8[:, ROW * i : ROW * i + V_SPLIT], in0=resf[:, i, 0:V_SPLIT], scalar1=fac[:, 0:1], scalar2=None, op0=ALU.mult, saturate=False
-            )
-            nc.scalar.activation(
-                out=res8[:, ROW * i + V_SPLIT : ROW * (i + 1)],
-                in_=resf[:, i, V_SPLIT:ROW],
-                func=ACT.Identity,
-                scale=fac[:, 0:1],
-                bias=zero1[:, 0:1],
-                saturate=False,
-            )
-            nc.sync.dma_start(out=o1[:, cuts[i] : cuts[i + 1]], in_=res8[:, cuts[i] : cuts[i + 1]].bitcast(U8))
+        nc.vector.reciprocal(out=fac[:], in_=s448[:])
+        flat = res[:].rearrange("p i h d -> p (i h d)")
+        for lo, hi in zip(CUTS[0:-1], CUTS[1:]):
+            mid = lo + (hi - lo) * 2 // 3 // 32 * 32
+            nc.vector.tensor_scalar(out=res8[:, lo:mid], in0=flat[:, lo:mid], scalar1=fac[:, 0:1], scalar2=None, op0=ALU.mult, saturate=False)
+            nc.scalar.activation(out=res8[:, mid:hi], in_=flat[:, mid:hi], func=ACT.Identity, scale=fac[:, 0:1], bias=zero1[:, 0:1], saturate=False)
+            nc.sync.dma_start(out=o1[:, lo:hi], in_=res8[:, lo:hi].bitcast(U8))

@@ -329,12 +329,14 @@ def tile_lorentzmla_pb_kernel(tc, x, freqs_cos, freqs_sin, wq_w, wq_b, out_0, ou
                 add_bias(c, i)
                 if i == 0 and c > 0:
                     rope_sin(c - 1, 1)
+                last = c == NCH - 1
                 if i == 1 and c > 0:
                     rope_cos(c - 1, 1, nc.gpsimd)
-                if i == 2:
+                if i == (1 if last else 2):
                     rope_sin(c, 0)
-                if i == 3:
+                if i == (1 if last else 3):
                     rope_cos(c, 0, nc.gpsimd)
+                if i == 3:
                     if c + 3 < NCH:
                         sort_words(("w", 3 * (c + 3)))
                 lag = 1 if c == NCH - 1 else 2

@@ -27,6 +27,7 @@ HD = QK + 1
 ROW = H * HD
 PASSES = 4
 FLOPS = 2 * TOK * H * QK * K
+ORDER = (0, 2, 4, 6, 1, 3, 5, 7)
 
 NCH = 8
 CW = 2 * QK
@@ -35,6 +36,13 @@ WIDTHS = (N_A, CW - N_A)
 RAW_BUFS = 10
 WARM = 6
 SORT_AHEAD = 2
+NU = 2
+V_ADD = ((7, 1),)
+STEPS = (("M", "Q", "B", "s1"), ("M", "B", "c1"), ("M", "Q", "B", "S0"), ("M", "B", "C0", "W"))
+LAST_STEPS = (("M", "B", "s1"), ("M", "B", "c1", "S0", "C0"), ("M", "B"), ("M", "B"))
+LAG = 2
+LAST_LAG = 1
+SUM_SLOTS = (0, 2)
 N_SORTED = 4
 CUTS = (0, 3584, 7168, 10240, 11776, NT * ROW)
 
@@ -72,6 +80,7 @@ def tile_lorentzmla_pb_kernel(tc, x, freqs_cos, freqs_sin, wq_w, wq_b, out_0, ou
         gwp = ctx.enter_context(tc.tile_pool(name="gwp", bufs=2))
         cdp = ctx.enter_context(tc.tile_pool(name="cdp", bufs=3))
         tmp = ctx.enter_context(tc.tile_pool(name="tmp", bufs=3))
+        usp = ctx.enter_context(tc.tile_pool(name="usp", bufs=NU))
         abp = ctx.enter_context(tc.tile_pool(name="abp", bufs=3))
         ps_t = ctx.enter_context(tc.psum_pool(name="ps_t", bufs=3))
         ps_a = ctx.enter_context(tc.psum_pool(name="ps_a", bufs=4))
@@ -94,7 +103,6 @@ def tile_lorentzmla_pb_kernel(tc, x, freqs_cos, freqs_sin, wq_w, wq_b, out_0, ou
         make_identity(nc, ident16[:])
         minus16 = const.tile([P, P], BF16, name="minus16")
         nc.gpsimd.tensor_scalar(out=minus16[:], in0=ident16[:], scalar1=-1.0, scalar2=0.0, op0=ALU.mult, op1=ALU.add)
-        u2 = [const.tile([P, 2, 2, QK], F32, name="u2_%d" % n) for n in range(2)]
 
         cos16 = const.tile([P, NT, 64], BF16, name="cos16")
         zsz = const.tile([P, 3, NT * 64], BF16, name="zsz")
@@ -110,8 +118,6 @@ def tile_lorentzmla_pb_kernel(tc, x, freqs_cos, freqs_sin, wq_w, wq_b, out_0, ou
         biasf = bias[:].rearrange("p h d -> p (h d)")
 
         tab = ps_c.tile([P, 2, NT, ROPE], BF16, name="tab")
-        for n in range(2):
-            nc.gpsimd.memset(u2[n][:], 0.0)
 
         res = const.tile([P, NT, H, HD], F32, name="res")
         resf = res[:].rearrange("p i h d -> p i (h d)")
@@ -131,6 +137,12 @@ def tile_lorentzmla_pb_kernel(tc, x, freqs_cos, freqs_sin, wq_w, wq_b, out_0, ou
         ab = {}
         state = {"loaded": 0, "summed": 0, "slot": 0}
         added = []
+        unquantized = []
+
+        def quantize_ready():
+            for part in unquantized:
+                quantize_w(part[0], part[1])
+            unquantized.clear()
 
         def load():
             n = state["loaded"]
@@ -141,12 +153,13 @@ def tile_lorentzmla_pb_kernel(tc, x, freqs_cos, freqs_sin, wq_w, wq_b, out_0, ou
             t = rawp.tile([P, K], BF16, name="raw", tag="raw")
             raw[(kind, r)] = t
             if n == 0:
-                nc.sync.dma_start(out=t[:, 0 : K // 2], in_=wq_w[0:P, 0 : K // 2])
-                nc.sync.dma_start(out=t[:, K // 2 : K], in_=wq_w[0:P, K // 2 : K])
+                nc.sync.dma_start(out=t[:, 0 : K // 2], in_=wq_w[CW * ORDER[0] : CW * ORDER[0] + P, 0 : K // 2])
+                nc.sync.dma_start(out=t[:, K // 2 : K], in_=wq_w[CW * ORDER[0] : CW * ORDER[0] + P, K // 2 : K])
             elif kind == "x":
                 nc.sync.dma_start(out=t[:], in_=xv[:, r, :])
             else:
-                nc.sync.dma_start(out=t[:], in_=wq_w[P * r : P * (r + 1), :])
+                row = CW * ORDER[r // 3] + P * (r % 3)
+                nc.sync.dma_start(out=t[:], in_=wq_w[row : row + P, :])
 
         def dummies(n):
             for d in range(n):
@@ -209,7 +222,7 @@ def tile_lorentzmla_pb_kernel(tc, x, freqs_cos, freqs_sin, wq_w, wq_b, out_0, ou
             if half == 1 and kind == "x":
                 quantize_x(r)
             elif half == 1 and r % 3 >= 1:
-                quantize_w(r // 3, r % 3 - 1)
+                unquantized.append((r // 3, r % 3 - 1))
 
         def bias_matmul(q):
             if q % 2 == 0:
@@ -252,38 +265,39 @@ def tile_lorentzmla_pb_kernel(tc, x, freqs_cos, freqs_sin, wq_w, wq_b, out_0, ou
                         stop=(g == PASSES - 1),
                     )
 
-        def add_bias(c, i):
-            if i % 2 == 0:
-                ab[(c, i // 2)] = abp.tile([P, 2, 2, QK], F32, name="ab", tag="ab")
-            nc.vector.tensor_tensor(
-                out=ab[(c, i // 2)][:, i % 2],
-                in0=acc[(c, i)][:].rearrange("p (h d) -> p h d", d=QK),
-                in1=bias[:, 2 * c : 2 * c + 2, :],
-                op=ALU.add,
-            )
+        us = {}
 
-        def rope_sin(c, k):
+        def add_bias(q, i):
+            h = slice(2 * ORDER[q], 2 * ORDER[q] + 2)
+            sums2 = acc[(q, i)][:].rearrange("p (h d) -> p h d", d=QK)
+            if i % 2 == 0:
+                ab[(q, i // 2)] = abp.tile([P, 2, 2, ROPE], F32, name="ab", tag="ab")
+            nc.vector.tensor_tensor(out=ab[(q, i // 2)][:, i % 2], in0=sums2[:, :, NOPE:QK], in1=bias[:, h, NOPE:QK], op=ALU.add)
+            nc.vector.tensor_tensor(out=res[:, i, h, 1 : 1 + NOPE], in0=sums2[:, :, 0:NOPE], in1=bias[:, h, 0:NOPE], op=ALU.add)
+
+        def rope_sin(q, k):
+            us[(q, k)] = usp.tile([P, 2, 2, ROPE], F32, name="us", tag="us")
             nc.vector.tensor_tensor(
-                out=u2[k][:, :, :, NOPE:QK].rearrange("p k h (j e) -> p k h j e", e=2),
-                in0=ab[(c, k)][:, :, :, NOPE:QK].rearrange("p k h (j e) -> p k h j e", e=2)[:, :, :, :, ::-1],
+                out=us[(q, k)][:].rearrange("p k h (j e) -> p k h j e", e=2),
+                in0=ab[(q, k)][:].rearrange("p k h (j e) -> p k h j e", e=2)[:, :, :, :, ::-1],
                 in1=tab[:, 1, 2 * k : 2 * k + 2].rearrange("p i (j e) -> p i j e", e=2).unsqueeze(2).to_broadcast([P, 2, 2, 64, 2]),
                 op=ALU.mult,
             )
 
-        def rope_cos(c, k, adder):
-            a = ab[(c, k)]
+        def rope_cos(q, k):
+            a = ab[(q, k)]
             nc.vector.tensor_tensor(
-                out=a[:, :, :, NOPE:QK],
-                in0=a[:, :, :, NOPE:QK],
-                in1=tab[:, 0, 2 * k : 2 * k + 2].unsqueeze(2).to_broadcast([P, 2, 2, ROPE]),
-                op=ALU.mult,
+                out=a[:], in0=a[:], in1=tab[:, 0, 2 * k : 2 * k + 2].unsqueeze(2).to_broadcast([P, 2, 2, ROPE]), op=ALU.mult
             )
-            adder.tensor_tensor(out=res[:, 2 * k : 2 * k + 2, 2 * c : 2 * c + 2, 1:HD], in0=a[:], in1=u2[k][:], op=ALU.add)
-            added.append((c, 2 * k, state["slot"]))
+            adder = nc.vector if (q, k) in V_ADD else nc.gpsimd
+            h = slice(2 * ORDER[q], 2 * ORDER[q] + 2)
+            adder.tensor_tensor(out=res[:, 2 * k : 2 * k + 2, h, 1 + NOPE : HD], in0=a[:], in1=us[(q, k)][:], op=ALU.add)
+            added.append((q, 2 * k, state["slot"]))
 
         def sums(n):
-            for c, i0, slot in added[state["summed"] : state["summed"] + n]:
+            for q, i0, slot in added[state["summed"] : state["summed"] + n]:
                 state["summed"] = state["summed"] + 1
+                c = ORDER[q]
                 for i in (i0, i0 + 1):
                     for h in (2 * c, 2 * c + 1):
                         junk = tmp.tile([P, QK], F32, name="junk", tag="junk")
@@ -291,8 +305,8 @@ def tile_lorentzmla_pb_kernel(tc, x, freqs_cos, freqs_sin, wq_w, wq_b, out_0, ou
                 nc.scalar.activation(
                     out=res[:, i0 : i0 + 2, 2 * c : 2 * c + 2, 0], in_=ssq[:, i0 : i0 + 2, 2 * c : 2 * c + 2], func=ACT.Sqrt, bias=1.0
                 )
-                lo = (CW + 2) * c // 8 * 8
-                hi = (CW + 2) * (c + 1) // 8 * 8
+                lo, hi = (CW + 2) * c, (CW + 2) * (c + 1)
+                lo, hi = (lo // 8 * 8, (hi + 7) // 8 * 8) if c % 2 == 1 else ((lo + 7) // 8 * 8, hi // 8 * 8)
                 for i in (i0, i0 + 1):
                     nc.sync.dma_start(out=o0[:, i, lo:hi], in_=resf[:, i, lo:hi])
 
@@ -314,36 +328,40 @@ def tile_lorentzmla_pb_kernel(tc, x, freqs_cos, freqs_sin, wq_w, wq_b, out_0, ou
                 table_matmul(n - 1)
             copies(t, 0)
             copies(t, 1)
+            quantize_ready()
             if n == 4:
                 nc.vector.tensor_copy(out=biasf[:, 0 : 2 * TOK], in_=spreadb[0][:])
         for k in (1, 2):
-            nc.scalar.copy(out=biasf[:, 2 * TOK * k : 2 * TOK * (k + 1)], in_=spreadb[k][:])
+            nc.vector.tensor_copy(out=biasf[:, 2 * TOK * k : 2 * TOK * (k + 1)], in_=spreadb[k][:])
         for c in range(NCH):
+            last = c == NCH - 1
             for i in range(NT):
                 for r, half in t_plan(c, i):
                     transposes(("w", r), half)
                 for r, half in t_plan(c, i):
                     copies(("w", r), half)
                 state["slot"] = NT * c + i
-                matmuls(c, i)
-                add_bias(c, i)
-                if i == 0 and c > 0:
-                    rope_sin(c - 1, 1)
-                last = c == NCH - 1
-                if i == 1 and c > 0:
-                    rope_cos(c - 1, 1, nc.gpsimd)
-                if i == (1 if last else 2):
-                    rope_sin(c, 0)
-                if i == (1 if last else 3):
-                    rope_cos(c, 0, nc.gpsimd)
-                if i == 3:
-                    if c + 3 < NCH:
-                        sort_words(("w", 3 * (c + 3)))
-                lag = 1 if c == NCH - 1 else 2
-                if (i % 2 == 0 or c == NCH - 1) and state["summed"] < len(added) and added[state["summed"]][2] + lag <= NT * c + i:
+                for step in (LAST_STEPS if last else STEPS)[i]:
+                    if step == "M":
+                        matmuls(c, i)
+                    elif step == "Q":
+                        quantize_ready()
+                    elif step == "B":
+                        add_bias(c, i)
+                    elif step == "W":
+                        if c + 3 < NCH:
+                            sort_words(("w", 3 * (c + 3)))
+                    else:
+                        q, k = (c if step[0] in "SC" else c - 1), int(step[1])
+                        if q >= 0:
+                            (rope_sin if step[0] in "Ss" else rope_cos)(q, k)
+                lag = LAST_LAG if last else LAG
+                while state["summed"] < len(added) and added[state["summed"]][2] + lag <= NT * c + i and (last or i in SUM_SLOTS):
                     sums(1)
+                    if not last:
+                        break
         rope_sin(NCH - 1, 1)
-        rope_cos(NCH - 1, 1, nc.vector)
+        rope_cos(NCH - 1, 1)
         sums(len(added))
 
         pmax = const.tile([P, 1], F32, name="pmax")

@@ -36,15 +36,19 @@ WIDTHS = (N_A, CW - N_A)
 RAW_BUFS = 10
 WARM = 6
 SORT_AHEAD = 2
+PRM = 5
 NU = 2
+V_COPIES = ()
+SPLIT = 2
+V_SQ = ()
 V_ADD = ((7, 1),)
-STEPS = (("M", "Q", "B", "s1"), ("M", "B", "c1"), ("M", "Q", "B", "S0"), ("M", "B", "C0", "W"))
-LAST_STEPS = (("M", "B", "s1"), ("M", "B", "c1", "S0", "C0"), ("M", "B"), ("M", "B"))
+STEPS = (("M", "w", "Q", "B", "s1"), ("M", "B", "c1"), ("M", "Q", "B", "S0"), ("M", "B", "C0"))
+LAST_STEPS = (("M", "B", "s1"), ("M", "B", "c1", "S0"), ("M", "B", "C0"), ("M", "B", "S1", "C1"))
 LAG = 2
 LAST_LAG = 1
 SUM_SLOTS = (0, 2)
 N_SORTED = 4
-CUTS = (0, 3584, 7168, 10240, 11776, NT * ROW)
+CUTS = (0, 3072, 6144, 9216, 11264, NT * ROW)
 
 HEAD = (("w", 0), ("w", 1), ("w", 2), ("x", 0), ("x", 1), ("x", 2), ("x", 3))
 
@@ -76,7 +80,7 @@ def tile_lorentzmla_pb_kernel(tc, x, freqs_cos, freqs_sin, wq_w, wq_b, out_0, ou
     with ExitStack() as ctx:
         const = ctx.enter_context(tc.tile_pool(name="const", bufs=1))
         rawp = ctx.enter_context(tc.tile_pool(name="rawp", bufs=RAW_BUFS))
-        prm = ctx.enter_context(tc.tile_pool(name="prm", bufs=4))
+        prm = ctx.enter_context(tc.tile_pool(name="prm", bufs=PRM))
         gwp = ctx.enter_context(tc.tile_pool(name="gwp", bufs=2))
         cdp = ctx.enter_context(tc.tile_pool(name="cdp", bufs=3))
         tmp = ctx.enter_context(tc.tile_pool(name="tmp", bufs=3))
@@ -215,7 +219,8 @@ def tile_lorentzmla_pb_kernel(tc, x, freqs_cos, freqs_sin, wq_w, wq_b, out_0, ou
                 key, col = ("w", r // 3, part), P * (r % 3 % 2)
                 if col == 0 and half == 0:
                     grouped[key] = gwp.tile([P, PASSES, WIDTHS[part], 4], BF16, name="gw%d" % part, tag="gw%d" % part, align_bytes=64)
-            nc.scalar.copy(
+            copy = nc.vector.tensor_copy if (t, half) in V_COPIES else nc.scalar.copy
+            copy(
                 out=grouped[key][:, 2 * half : 2 * half + 2, col : col + P, :].bitcast(F32),
                 in_=banks[(t, half)][:].rearrange("p a u r -> p a r u"),
             )
@@ -291,7 +296,10 @@ def tile_lorentzmla_pb_kernel(tc, x, freqs_cos, freqs_sin, wq_w, wq_b, out_0, ou
             )
             adder = nc.vector if (q, k) in V_ADD else nc.gpsimd
             h = slice(2 * ORDER[q], 2 * ORDER[q] + 2)
-            adder.tensor_tensor(out=res[:, 2 * k : 2 * k + 2, h, 1 + NOPE : HD], in0=a[:], in1=us[(q, k)][:], op=ALU.add)
+            n = SPLIT if (q, k) == (NCH - 1, 1) else 1
+            for e in range(n):
+                i0, i1 = 2 // n * e, 2 // n * (e + 1)
+                adder.tensor_tensor(out=res[:, 2 * k + i0 : 2 * k + i1, h, 1 + NOPE : HD], in0=a[:, i0:i1], in1=us[(q, k)][:, i0:i1], op=ALU.add)
             added.append((q, 2 * k, state["slot"]))
 
         def sums(n):
@@ -299,6 +307,12 @@ def tile_lorentzmla_pb_kernel(tc, x, freqs_cos, freqs_sin, wq_w, wq_b, out_0, ou
                 state["summed"] = state["summed"] + 1
                 c = ORDER[q]
                 for i in (i0, i0 + 1):
+                    if q == NCH - 1 and i in V_SQ:
+                        h = slice(2 * c, 2 * c + 2)
+                        sq = tmp.tile([P, 2, QK], F32, name="sq", tag="sq")
+                        nc.vector.tensor_tensor(out=sq[:], in0=res[:, i, h, 1:HD], in1=res[:, i, h, 1:HD], op=ALU.mult)
+                        nc.vector.tensor_reduce(out=ssq[:, i, h], in_=sq[:], axis=AX.X, op=ALU.add)
+                        continue
                     for h in (2 * c, 2 * c + 1):
                         junk = tmp.tile([P, QK], F32, name="junk", tag="junk")
                         nc.scalar.activation(out=junk[:], in_=res[:, i, h, 1:HD], func=ACT.Square, accum_out=ssq[:, i, h : h + 1])
@@ -348,6 +362,9 @@ def tile_lorentzmla_pb_kernel(tc, x, freqs_cos, freqs_sin, wq_w, wq_b, out_0, ou
                         quantize_ready()
                     elif step == "B":
                         add_bias(c, i)
+                    elif step == "w":
+                        if c + 2 < NCH:
+                            sort_words(("w", 3 * (c + 2)))
                     elif step == "W":
                         if c + 3 < NCH:
                             sort_words(("w", 3 * (c + 3)))
@@ -360,8 +377,6 @@ def tile_lorentzmla_pb_kernel(tc, x, freqs_cos, freqs_sin, wq_w, wq_b, out_0, ou
                     sums(1)
                     if not last:
                         break
-        rope_sin(NCH - 1, 1)
-        rope_cos(NCH - 1, 1)
         sums(len(added))
 
         pmax = const.tile([P, 1], F32, name="pmax")

@@ -34,7 +34,7 @@ CW = 2 * QK
 N_A = 256
 WIDTHS = (N_A, CW - N_A)
 RAW_BUFS = 10
-WARM = 6
+WARM = 4
 SORT_AHEAD = 2
 PRM = 5
 NU = 2
@@ -55,13 +55,8 @@ HEAD = (("w", 0), ("w", 1), ("w", 2), ("x", 0), ("x", 1), ("x", 2), ("x", 3))
 
 def t_plan(c, i):
     slot = NT * c + i
-    if 1 <= slot <= 3:
-        n = slot - 1
-    elif slot >= 4 and slot % 2 == 0:
-        n = slot // 2 + 1
-    else:
-        return ()
-    if n >= 2 * (NCH - 1):
+    n = 0 if slot == 1 else slot // 2
+    if slot == 0 or (slot > 1 and slot % 2 == 1) or n >= 2 * (NCH - 1):
         return ()
     r = 3 * (1 + n // 2)
     if n % 2 == 0:

from contextlib import ExitStack

import concourse.mybir as mybir
from concourse.masks import make_identity

F32 = mybir.dt.float32
BF16 = mybir.dt.bfloat16
U32 = mybir.dt.uint32
U8 = mybir.dt.uint8
I32 = mybir.dt.int32
FP8X4 = mybir.dt.float8_e4m3fn_x4
FP8 = mybir.dt.float8_e4m3fn
ALU = mybir.AluOpType
ACT = mybir.ActivationFunctionType
AX = mybir.AxisListType

P = 128
K = 2048
KW = K // 2
TOK = 512
NT = 4
H = 16
NOPE = 64
ROPE = 128
QK = NOPE + ROPE
HD = QK + 1
ROW = H * HD
PASSES = 4
FLOPS = 2 * TOK * H * QK * K
ORDER = (0, 2, 4, 6, 1, 3, 5, 7)

NCH = 8
CW = 2 * QK
N_A = 256
WIDTHS = (N_A, CW - N_A)
RAW_BUFS = 10
WARM = 4
SORT_AHEAD = 2
PRM = 5
NU = 2
V_COPIES = ()
SPLIT = 2
V_SQ = ()
V_ADD = ((7, 1),)
STEPS = (("M", "w", "Q", "B", "s1"), ("M", "B", "c1"), ("M", "Q", "B", "S0"), ("M", "B", "C0"))
LAST_STEPS = (("M", "B", "s1"), ("M", "B", "c1", "S0"), ("M", "B", "C0"), ("M", "B", "S1", "C1"))
LAG = 2
LAST_LAG = 1
SUM_SLOTS = (0, 2)
N_SORTED = 4
CUTS = (0, 3072, 6144, 9216, 11264, NT * ROW)

HEAD = (("w", 0), ("w", 1), ("w", 2), ("x", 0), ("x", 1), ("x", 2), ("x", 3))


def t_plan(c, i):
    slot = NT * c + i
    n = 0 if slot == 1 else slot // 2
    if slot == 0 or (slot > 1 and slot % 2 == 1) or n >= 2 * (NCH - 1):
        return ()
    r = 3 * (1 + n // 2)
    if n % 2 == 0:
        return ((r, 0), (r, 1), (r + 1, 0))
    return ((r + 1, 1), (r + 2, 0), (r + 2, 1))


def tile_lorentzmla_pb_kernel(tc, x, freqs_cos, freqs_sin, wq_w, wq_b, out_0, out_1):
    nc = tc.nc
    xv = x.rearrange("b s k -> (b s) k").rearrange("(p i) k -> p i k", i=NT)
    o0 = out_0.rearrange("b s h d -> (b s) (h d)").rearrange("(p i) e -> p i e", i=NT)
    o1 = out_1.rearrange("b s h d -> (b s) (h d)").rearrange("(p i) e -> p (i e)", i=NT)
    cosv = freqs_cos.rearrange("(q i) j -> q i j", i=NT)
    sinv = freqs_sin.rearrange("(q i) j -> q i j", i=NT)

    with ExitStack() as ctx:
        const = ctx.enter_context(tc.tile_pool(name="const", bufs=1))
        rawp = ctx.enter_context(tc.tile_pool(name="rawp", bufs=RAW_BUFS))
        prm = ctx.enter_context(tc.tile_pool(name="prm", bufs=PRM))
        gwp = ctx.enter_context(tc.tile_pool(name="gwp", bufs=2))
        cdp = ctx.enter_context(tc.tile_pool(name="cdp", bufs=3))
        tmp = ctx.enter_context(tc.tile_pool(name="tmp", bufs=3))
        usp = ctx.enter_context(tc.tile_pool(name="usp", bufs=NU))
        abp = ctx.enter_context(tc.tile_pool(name="abp", bufs=3))
        ps_t = ctx.enter_context(tc.psum_pool(name="ps_t", bufs=3))
        ps_a = ctx.enter_context(tc.psum_pool(name="ps_a", bufs=4))
        ps_c = ctx.enter_context(tc.psum_pool(name="ps_c", bufs=1))
        ctx.enter_context(tc.manual_schedule())

        one1 = const.tile([P, 1], F32, name="one1")
        nc.vector.memset(one1[:], 1.0)
        zero1 = const.tile([P, 1], F32, name="zero1")
        nc.vector.memset(zero1[:], 0.0)
        dummy = const.tile([P, TOK], BF16, name="dummy")
        nc.vector.memset(dummy[:].bitcast(I32), 0)
        brow = const.tile([P, H * QK], BF16, name="brow")
        nc.vector.memset(brow[:].bitcast(I32), 0)
        ones = const.tile([P, P], BF16, name="ones")
        nc.vector.memset(ones[:], 1.0)
        ident = const.tile([P, P], F32, name="ident")
        make_identity(nc, ident[:])
        ident16 = const.tile([P, P], BF16, name="ident16")
        make_identity(nc, ident16[:])
        minus16 = const.tile([P, P], BF16, name="minus16")
        nc.gpsimd.tensor_scalar(out=minus16[:], in0=ident16[:], scalar1=-1.0, scalar2=0.0, op0=ALU.mult, op1=ALU.add)

        cos16 = const.tile([P, NT, 64], BF16, name="cos16")
        zsz = const.tile([P, 3, NT * 64], BF16, name="zsz")
        nc.vector.memset(zsz[:, 0, :].bitcast(I32), 0)
        nc.vector.memset(zsz[:, 2, :].bitcast(I32), 0)
        for half in range(2):
            nc.scalar.dma_start(out=cos16[64 * half : 64 * half + 64], in_=cosv)
            nc.scalar.dma_start(out=zsz[64 * half : 64 * half + 64, 1, :].rearrange("p (i j) -> p i j", i=NT), in_=sinv)
        warm = const.tile([P, 1], F32, name="warm")
        nc.scalar.activation(out=warm[:], in_=one1[:], func=ACT.Sqrt)
        nc.scalar.dma_start(out=brow[0:1, :], in_=wq_b.rearrange("(o n) -> o n", o=1))
        bias = const.tile([P, H, QK], BF16, name="bias")
        biasf = bias[:].rearrange("p h d -> p (h d)")

        tab = ps_c.tile([P, 2, NT, ROPE], BF16, name="tab")

        res = const.tile([P, NT, H, HD], F32, name="res")
        resf = res[:].rearrange("p i h d -> p i (h d)")
        res8 = const.tile([P, NT * ROW], FP8, name="res8")
        ssq = const.tile([P, NT, H], F32, name="ssq")
        x_codes = const.tile([P, NT, PASSES, P], U32, name="x_codes", align_bytes=64)
        x_scales = const.tile([P, NT, PASSES, P], U8, name="x_scales", align_bytes=64)

        order = list(HEAD) + [("w", r) for r in range(3, 3 * NCH)]
        raw = {}
        sorted_tiles = {}
        spreadb = {}
        banks = {}
        grouped = {}
        codes = {}
        acc = {}
        ab = {}
        state = {"loaded": 0, "summed": 0, "slot": 0}
        added = []
        unquantized = []

        def quantize_ready():
            for part in unquantized:
                quantize_w(part[0], part[1])
            unquantized.clear()

        def load():
            n = state["loaded"]
            if n >= len(order):
                return
            state["loaded"] = n + 1
            kind, r = order[n]
            t = rawp.tile([P, K], BF16, name="raw", tag="raw")
            raw[(kind, r)] = t
            if n == 0:
                nc.sync.dma_start(out=t[:, 0 : K // 2], in_=wq_w[CW * ORDER[0] : CW * ORDER[0] + P, 0 : K // 2])
                nc.sync.dma_start(out=t[:, K // 2 : K], in_=wq_w[CW * ORDER[0] : CW * ORDER[0] + P, K // 2 : K])
            elif kind == "x":
                nc.sync.dma_start(out=t[:], in_=xv[:, r, :])
            else:
                row = CW * ORDER[r // 3] + P * (r % 3)
                nc.sync.dma_start(out=t[:], in_=wq_w[row : row + P, :])

        def dummies(n):
            for d in range(n):
                sink = ps_a.tile([P, TOK], F32, name="sink", tag="acc")
                nc.tensor.matmul(out=sink[:], lhsT=dummy[:, 0:P], rhs=dummy[:], start=True, stop=True)

        def sort_words(t):
            srt = prm.tile([P, 2, KW // 2], F32, name="srt", tag="srt")
            nc.vector.tensor_copy(out=srt[:], in_=raw[t][:].bitcast(F32).rearrange("p (w u) -> p u w", u=2))
            sorted_tiles[t] = srt

        def transposes(t, half):
            words = raw[t][:].bitcast(F32)
            xt = ps_t.tile([P, 2, 2, P], F32, name="xt", tag="xt")
            for a in range(2):
                g = 2 * half + a
                for u in range(2):
                    if t in sorted_tiles:
                        src = sorted_tiles[t][:, u, P * g : P * (g + 1)]
                    else:
                        src = words[:, 256 * g + u : 256 * (g + 1) : 2]
                    nc.tensor.transpose(xt[:, a, u, :], src, ident[:])
            banks[(t, half)] = xt
            if half == 1:
                load()

        def quantize_x(i):
            nc.vector.quantize_mx(
                out=x_codes[:, i].rearrange("p g n -> p (g n)").bitcast(FP8X4),
                scales=x_scales[:, i].rearrange("p g n -> p (g n)"),
                in_=grouped[("x", i)][:].rearrange("p g n t -> p (g n t)"),
            )

        def quantize_w(c, part):
            width = WIDTHS[part]
            wc = cdp.tile([P, PASSES, width], U32, name="w_codes%d" % part, tag="w_codes%d" % part, align_bytes=64)
            ws = cdp.tile([P, PASSES, width], U8, name="w_scales%d" % part, tag="w_scales%d" % part, align_bytes=64)
            codes[(c, part)] = (wc, ws)
            nc.vector.quantize_mx(
                out=wc[:].rearrange("p g n -> p (g n)").bitcast(FP8X4),
                scales=ws[:].rearrange("p g n -> p (g n)"),
                in_=grouped[("w", c, part)][:].rearrange("p g n t -> p (g n t)"),
            )

        def copies(t, half):
            kind, r = t
            if kind == "x":
                key, col = ("x", r), 0
                if half == 0:
                    grouped[key] = gwp.tile([P, PASSES, P, 4], BF16, name="gx", tag="gx", align_bytes=64)
            else:
                part = r % 3 // 2
                key, col = ("w", r // 3, part), P * (r % 3 % 2)
                if col == 0 and half == 0:
                    grouped[key] = gwp.tile([P, PASSES, WIDTHS[part], 4], BF16, name="gw%d" % part, tag="gw%d" % part, align_bytes=64)
            copy = nc.vector.tensor_copy if (t, half) in V_COPIES else nc.scalar.copy
            copy(
                out=grouped[key][:, 2 * half : 2 * half + 2, col : col + P, :].bitcast(F32),
                in_=banks[(t, half)][:].rearrange("p a u r -> p a r u"),
            )
            if half == 1 and kind == "x":
                quantize_x(r)
            elif half == 1 and r % 3 >= 1:
                unquantized.append((r // 3, r % 3 - 1))

        def bias_matmul(q):
            if q % 2 == 0:
                spreadb[q // 2] = ps_a.tile([P, 2 * TOK], BF16, name="pb", tag="acc")
            nc.tensor.matmul(
                out=spreadb[q // 2][:, TOK * (q % 2) : TOK * (q % 2 + 1)], lhsT=ones[:], rhs=brow[:, TOK * q : TOK * (q + 1)], start=True, stop=True
            )

        def table_matmul(n):
            if n == 0:
                nc.tensor.matmul(
                    out=tab[:, 0].rearrange("p i (j e) -> p (i j) e", e=2),
                    lhsT=ident16[:],
                    rhs=cos16[:].rearrange("p i j -> p (i j)").unsqueeze(2).to_broadcast([P, NT * 64, 2]),
                    start=True,
                    stop=True,
                )
            else:
                nc.tensor.matmul(
                    out=tab[:, 1].rearrange("p i (j e) -> p (i j) e", e=2),
                    lhsT=(ident16, minus16)[n - 1][:],
                    rhs=zsz[:, n - 1 : n + 1, :].rearrange("p e n -> p n e"),
                    start=(n == 1),
                    stop=(n == 2),
                )

        def matmuls(c, i):
            a = ps_a.tile([P, CW], F32, name="acc", tag="acc")
            acc[(c, i)] = a
            for part in range(2):
                wc, ws = codes[(c, part)]
                for g in range(PASSES):
                    nc.tensor.matmul_mx(
                        out=a[:, N_A * part : N_A * part + WIDTHS[part]],
                        lhsT=x_codes[:, i, g, :].bitcast(FP8X4),
                        lhsT_scale=x_scales[:, i, g, :],
                        rhs=wc[:, g, :].bitcast(FP8X4),
                        rhs_scale=ws[:, g, :],
                        start=(g == 0),
                        stop=(g == PASSES - 1),
                    )

        us = {}

        def add_bias(q, i):
            h = slice(2 * ORDER[q], 2 * ORDER[q] + 2)
            sums2 = acc[(q, i)][:].rearrange("p (h d) -> p h d", d=QK)
            if i % 2 == 0:
                ab[(q, i // 2)] = abp.tile([P, 2, 2, ROPE], F32, name="ab", tag="ab")
            nc.vector.tensor_tensor(out=ab[(q, i // 2)][:, i % 2], in0=sums2[:, :, NOPE:QK], in1=bias[:, h, NOPE:QK], op=ALU.add)
            nc.vector.tensor_tensor(out=res[:, i, h, 1 : 1 + NOPE], in0=sums2[:, :, 0:NOPE], in1=bias[:, h, 0:NOPE], op=ALU.add)

        def rope_sin(q, k):
            us[(q, k)] = usp.tile([P, 2, 2, ROPE], F32, name="us", tag="us")
            nc.vector.tensor_tensor(
                out=us[(q, k)][:].rearrange("p k h (j e) -> p k h j e", e=2),
                in0=ab[(q, k)][:].rearrange("p k h (j e) -> p k h j e", e=2)[:, :, :, :, ::-1],
                in1=tab[:, 1, 2 * k : 2 * k + 2].rearrange("p i (j e) -> p i j e", e=2).unsqueeze(2).to_broadcast([P, 2, 2, 64, 2]),
                op=ALU.mult,
            )

        def rope_cos(q, k):
            a = ab[(q, k)]
            nc.vector.tensor_tensor(
                out=a[:], in0=a[:], in1=tab[:, 0, 2 * k : 2 * k + 2].unsqueeze(2).to_broadcast([P, 2, 2, ROPE]), op=ALU.mult
            )
            adder = nc.vector if (q, k) in V_ADD else nc.gpsimd
            h = slice(2 * ORDER[q], 2 * ORDER[q] + 2)
            n = SPLIT if (q, k) == (NCH - 1, 1) else 1
            for e in range(n):
                i0, i1 = 2 // n * e, 2 // n * (e + 1)
                adder.tensor_tensor(out=res[:, 2 * k + i0 : 2 * k + i1, h, 1 + NOPE : HD], in0=a[:, i0:i1], in1=us[(q, k)][:, i0:i1], op=ALU.add)
            added.append((q, 2 * k, state["slot"]))

        def sums(n):
            for q, i0, slot in added[state["summed"] : state["summed"] + n]:
                state["summed"] = state["summed"] + 1
                c = ORDER[q]
                for i in (i0, i0 + 1):
                    if q == NCH - 1 and i in V_SQ:
                        h = slice(2 * c, 2 * c + 2)
                        sq = tmp.tile([P, 2, QK], F32, name="sq", tag="sq")
                        nc.vector.tensor_tensor(out=sq[:], in0=res[:, i, h, 1:HD], in1=res[:, i, h, 1:HD], op=ALU.mult)
                        nc.vector.tensor_reduce(out=ssq[:, i, h], in_=sq[:], axis=AX.X, op=ALU.add)
                        continue
                    for h in (2 * c, 2 * c + 1):
                        junk = tmp.tile([P, QK], F32, name="junk", tag="junk")
                        nc.scalar.activation(out=junk[:], in_=res[:, i, h, 1:HD], func=ACT.Square, accum_out=ssq[:, i, h : h + 1])
                nc.scalar.activation(
                    out=res[:, i0 : i0 + 2, 2 * c : 2 * c + 2, 0], in_=ssq[:, i0 : i0 + 2, 2 * c : 2 * c + 2], func=ACT.Sqrt, bias=1.0
                )
                lo, hi = (CW + 2) * c, (CW + 2) * (c + 1)
                lo, hi = (lo // 8 * 8, (hi + 7) // 8 * 8) if c % 2 == 1 else ((lo + 7) // 8 * 8, hi // 8 * 8)
                for i in (i0, i0 + 1):
                    nc.sync.dma_start(out=o0[:, i, lo:hi], in_=resf[:, i, lo:hi])

        for n in range(RAW_BUFS):
            load()
        dummies(WARM)
        for t in HEAD[0:SORT_AHEAD]:
            sort_words(t)
        for n, t in enumerate(HEAD):
            if n + SORT_AHEAD < N_SORTED:
                sort_words(HEAD[n + SORT_AHEAD])
            transposes(t, 0)
            transposes(t, 1)
            if n == 0:
                dummies(1)
            else:
                bias_matmul(n - 1)
            if 1 <= n <= 3:
                table_matmul(n - 1)
            copies(t, 0)
            copies(t, 1)
            quantize_ready()
            if n == 4:
                nc.vector.tensor_copy(out=biasf[:, 0 : 2 * TOK], in_=spreadb[0][:])
        for k in (1, 2):
            nc.vector.tensor_copy(out=biasf[:, 2 * TOK * k : 2 * TOK * (k + 1)], in_=spreadb[k][:])
        for c in range(NCH):
            last = c == NCH - 1
            for i in range(NT):
                for r, half in t_plan(c, i):
                    transposes(("w", r), half)
                for r, half in t_plan(c, i):
                    copies(("w", r), half)
                state["slot"] = NT * c + i
                for step in (LAST_STEPS if last else STEPS)[i]:
                    if step == "M":
                        matmuls(c, i)
                    elif step == "Q":
                        quantize_ready()
                    elif step == "B":
                        add_bias(c, i)
                    elif step == "w":
                        if c + 2 < NCH:
                            sort_words(("w", 3 * (c + 2)))
                    elif step == "W":
                        if c + 3 < NCH:
                            sort_words(("w", 3 * (c + 3)))
                    else:
                        q, k = (c if step[0] in "SC" else c - 1), int(step[1])
                        if q >= 0:
                            (rope_sin if step[0] in "Ss" else rope_cos)(q, k)
                lag = LAST_LAG if last else LAG
                while state["summed"] < len(added) and added[state["summed"]][2] + lag <= NT * c + i and (last or i in SUM_SLOTS):
                    sums(1)
                    if not last:
                        break
        sums(len(added))

        pmax = const.tile([P, 1], F32, name="pmax")
        nc.vector.tensor_reduce(out=pmax[:], in_=res[:].rearrange("p i h d -> p (i h) d")[:, :, 0], axis=AX.X, op=ALU.max)
        spread = ps_t.tile([P, P], F32, name="spread", tag="xt")
        nc.tensor.transpose(spread[:], pmax[:, 0:1].to_broadcast([P, P]), ident[:])
        scaled = const.tile([P, P], F32, name="scaled")
        s448 = const.tile([P, 1], F32, name="s448")
        nc.vector.tensor_scalar(out=scaled[:], in0=spread[:], scalar1=1.0 / 448.0, scalar2=None, op0=ALU.mult, op1=ALU.max, accum_out=s448[:])
        fac = const.tile([P, 1], F32, name="fac")
        nc.vector.reciprocal(out=fac[:], in_=s448[:])
        flat = res[:].rearrange("p i h d -> p (i h d)")
        for lo, hi in zip(CUTS[0:-1], CUTS[1:]):
            mid = lo + (hi - lo) * 2 // 3 // 32 * 32
            nc.vector.tensor_scalar(out=res8[:, lo:mid], in0=flat[:, lo:mid], scalar1=fac[:, 0:1], scalar2=None, op0=ALU.mult, saturate=False)
            nc.scalar.activation(out=res8[:, mid:hi], in_=flat[:, mid:hi], func=ACT.Identity, scale=fac[:, 0:1], bias=zero1[:, 0:1], saturate=False)
            nc.sync.dma_start(out=o1[:, lo:hi], in_=res8[:, lo:hi].bitcast(U8))
